import numpy as np
import ml_dtypes


def mxq(x, axis, fmt="e4m3"):
    dtype, down = {"e4m3": (ml_dtypes.float8_e4m3fn, 7), "e5m2": (ml_dtypes.float8_e5m2, 14)}[fmt]
    v = np.moveaxis(np.asarray(x, np.float32).astype(ml_dtypes.bfloat16).astype(np.float64), axis, -1)
    blocks = v.reshape(v.shape[:-1] + (-1, 32))
    amax = np.abs(blocks).max(-1, keepdims=True)
    byte = np.maximum(np.where(amax > 0, np.frexp(amax)[1] - 1 + 127, 0) - down, 1)
    scale = np.exp2(byte - 127.0)
    codes = (blocks / scale).astype(np.float32).astype(dtype).astype(np.float64)
    return np.moveaxis((codes * scale).reshape(v.shape), -1, axis)


BF16 = ml_dtypes.bfloat16


def bf(x):
    return np.asarray(x, np.float32).astype(BF16)


def f64(x):
    return np.asarray(x).astype(np.float64)


B, C, PPC, D, R = 16384, 16, 8, 1024, 8
P = C * PPC


def setup_inputs():
    u = np.random.standard_normal((R, D))
    g = 0.5 / np.sqrt(D)
    x = (np.random.standard_normal((B, R)) @ u + np.random.standard_normal((B, D))) * g
    prototypes = (np.random.standard_normal((P, R)) @ u + np.random.standard_normal((P, D))) * g
    return {"x": bf(x), "prototypes": bf(prototypes)}


def reference(x, prototypes):
    x, prototypes = f64(x), f64(prototypes)
    x2 = np.sum(x * x, axis=1, keepdims=True)
    p2 = np.sum(prototypes * prototypes, axis=1)
    sq = x2 + p2[None, :] - 2.0 * (mxq(x, 1, "e4m3") @ mxq(prototypes, 1, "e4m3").T)
    dists = np.sqrt(np.maximum(sq, 0.0))
    logits = -dists
    return np.max(logits.reshape(x.shape[0], C, PPC), axis=2)

@@ -1,0 +1,164 @@
+from contextlib import ExitStack
+
+import concourse.mybir as mybir
+from concourse.masks import make_identity
+
+F32 = mybir.dt.float32
+BF16 = mybir.dt.bfloat16
+U32 = mybir.dt.uint32
+U8 = mybir.dt.uint8
+FP8X4 = mybir.dt.float8_e4m3fn_x4
+ALU = mybir.AluOpType
+ACT = mybir.ActivationFunctionType
+AX = mybir.AxisListType
+
+B, D, NP, NC, PPC = 16384, 1024, 128, 16, 8
+P = 128
+NT = B // P
+GT = 4
+NG = NT // GT
+W = D // 2
+
+FLOPS = 2 * B * NP * D
+
+TINY = 2.0 ** -116
+SQRT_TINY = 2.0 ** -58
+
+BATCHES = [(0, 32), (32, 32), (64, 32), (96, 24), (120, 8)]
+
+
+def tile_lvq_t_kernel(tc, x, prototypes, out):
+    nc = tc.nc
+    xv = x.rearrange("(p t) k -> p (t k)", t=NT)
+    outv = out.rearrange("(p t) c -> p (t c)", t=NT)
+
+    with ExitStack() as ctx:
+        const = ctx.enter_context(tc.tile_pool(name="const", bufs=1))
+        xpool = ctx.enter_context(tc.tile_pool(name="xpool", bufs=8))
+        work = ctx.enter_context(tc.tile_pool(name="work", bufs=3))
+        fin = ctx.enter_context(tc.tile_pool(name="fin", bufs=2))
+        pxt = ctx.enter_context(tc.psum_pool(name="pxt", bufs=5))
+        pacc = ctx.enter_context(tc.psum_pool(name="pacc", bufs=2))
+        pset = ctx.enter_context(tc.psum_pool(name="pset", bufs=1))
+
+        warm = const.tile([P, 1], F32, name="warm")
+        nc.vector.memset(warm[:], 1.0)
+        warm2 = const.tile([P, 1], F32, name="warm2")
+        nc.scalar.activation(out=warm2[:], in_=warm[:], func=ACT.Sqrt)
+
+        ident = const.tile([P, P], F32, name="ident")
+        make_identity(nc, ident[:])
+        ones = const.tile([P, P], F32, name="ones")
+        nc.vector.memset(ones[:], 1.0)
+
+        x2 = const.tile([P, NT], F32, name="x2")
+        mn = const.tile([P, NT * NC], F32, name="mn")
+
+        def transpose_words(src32, dst):
+            for q in range(4):
+                nc.tensor.transpose(dst[:, q * P:(q + 1) * P], src32[:, q * P:(q + 1) * P], ident[:])
+
+        def evacuate(eng_copy, dst32, src):
+            eng_copy(
+                out=dst32.rearrange("p (g b u) -> p g b u", g=2, u=2),
+                in_=src.rearrange("p (g u b) -> p g b u", g=2, u=2),
+            )
+
+        pr = const.tile([P, D], BF16, name="pr")
+        nc.sync.dma_start(out=pr[:], in_=prototypes)
+        pjunk = const.tile([P, D], BF16, name="pjunk")
+        p2 = const.tile([P, 1], F32, name="p2")
+        nc.scalar.activation(out=pjunk[:], in_=pr[:], func=ACT.Square, accum_out=p2[:])
+        p2rep = const.tile([P, P], F32, name="p2rep")
+        nc.vector.tensor_scalar_mul(out=p2rep[:], in0=ones[:], scalar1=p2[:, 0:1])
+        p2t = pset.tile([P, P], F32, name="p2t")
+        nc.tensor.transpose(p2t[:], p2rep[:], ident[:])
+        p2b = const.tile([P, P], F32, name="p2b")
+        nc.vector.tensor_copy(out=p2b[:], in_=p2t[:])
+
+        pxtile = pxt.tile([P, W], F32, name="xt", tag="xt")
+        transpose_words(pr[:].bitcast(F32), pxtile)
+        pgrp = const.tile([P, D], BF16, name="pgrp", align_bytes=64)
+        evacuate(nc.vector.tensor_copy, pgrp[:].bitcast(F32), pxtile[:])
+        pcodes = const.tile([P, D // 4], U32, name="pcodes", align_bytes=64)
+        pscl = const.tile([P, D // 4], U8, name="pscl", align_bytes=64)
+        nc.vector.quantize_mx(out=pcodes[:].bitcast(FP8X4), scales=pscl[:], in_=pgrp[:])
+
+        state = {}
+
+        def stage_a(g):
+            xs = xpool.tile([P, GT * D], BF16, name="xs", tag="xs")
+            nc.sync.dma_start(out=xs[:], in_=xv[:, g * GT * D:(g + 1) * GT * D])
+            xs32 = xs[:].bitcast(F32)
+            grp = work.tile([P, GT * D], BF16, name="grp", tag="grp", align_bytes=64)
+            grp32 = grp[:].bitcast(F32)
+            for j in range(GT):
+                t = g * GT + j
+                junk = work.tile([P, D], BF16, name="junk", tag="junk")
+                nc.scalar.activation(
+                    out=junk[:], in_=xs[:, j * D:(j + 1) * D], func=ACT.Square, accum_out=x2[:, t:t + 1]
+                )
+                xt = pxt.tile([P, W], F32, name="xt", tag="xt")
+                transpose_words(xs32[:, j * W:(j + 1) * W], xt)
+                evacuate(nc.vector.tensor_copy, grp32[:, j * W:(j + 1) * W], xt[:])
+            state[g] = grp
+
+        def stage_b(g):
+            grp = state[g]
+            codes = work.tile([P, GT * D // 4], U32, name="codes", tag="codes", align_bytes=64)
+            scl = work.tile([P, GT * D // 4], U8, name="scl", tag="scl", align_bytes=64)
+            nc.vector.quantize_mx(out=codes[:].bitcast(FP8X4), scales=scl[:], in_=grp[:])
+            acc = pacc.tile([P, GT * NP], F32, name="acc", tag="acc")
+            for j in range(GT):
+                for h in range(2):
+                    c0 = (j * 2 + h) * P
+                    nc.tensor.matmul_mx(
+                        out=acc[:, j * NP:(j + 1) * NP],
+                        lhsT=codes[:, c0:c0 + P].bitcast(FP8X4),
+                        lhsT_scale=scl[:, c0:c0 + P],
+                        rhs=pcodes[:, h * NP:(h + 1) * NP].bitcast(FP8X4),
+                        rhs_scale=pscl[:, h * NP:(h + 1) * NP],
+                        start=(h == 0),
+                        stop=(h == 1),
+                    )
+            tt = work.tile([P, GT * NP], F32, name="tt", tag="tt")
+            nc.vector.scalar_tensor_tensor(
+                out=tt[:].rearrange("p (j n) -> p j n", j=GT),
+                in0=acc[:].rearrange("p (j n) -> p j n", j=GT),
+                scalar=-2.0,
+                in1=p2b[:].unsqueeze(1).to_broadcast([P, GT, NP]),
+                op0=ALU.mult,
+                op1=ALU.add,
+            )
+            nc.vector.tensor_reduce(
+                out=mn[:, g * GT * NC:(g + 1) * GT * NC],
+                in_=tt[:].rearrange("p (m q) -> p m q", q=PPC),
+                axis=AX.X,
+                op=ALU.min,
+            )
+
+        def finish(t0, n):
+            s = fin.tile([P, n * NC], F32, name="s", tag="s")
+            nc.vector.tensor_tensor(
+                out=s[:].rearrange("p (t c) -> p t c", c=NC),
+                in0=mn[:, t0 * NC:(t0 + n) * NC].rearrange("p (t c) -> p t c", c=NC),
+                in1=x2[:, t0:t0 + n].unsqueeze(2).to_broadcast([P, n, NC]),
+                op=ALU.add,
+            )
+            nc.vector.tensor_scalar_max(out=s[:], in0=s[:], scalar1=TINY)
+            r = fin.tile([P, n * NC], F32, name="r", tag="r")
+            nc.scalar.activation(out=r[:], in_=s[:], func=ACT.Sqrt)
+            res = fin.tile([P, n * NC], F32, name="res", tag="res")
+            nc.vector.tensor_scalar(
+                out=res[:], in0=r[:], scalar1=SQRT_TINY, scalar2=-1.0, op0=ALU.subtract, op1=ALU.mult
+            )
+            nc.sync.dma_start(out=outv[:, t0 * NC:(t0 + n) * NC], in_=res[:])
+
+        ends = dict(((t0 + n) // GT - 1, (t0, n)) for (t0, n) in BATCHES)
+        for i in range(NG + 1):
+            if i < NG:
+                stage_a(i)
+            if i >= 1:
+                stage_b(i - 1)
+                if (i - 1) in ends:
+                    finish(*ends[i - 1])

@@ -18,13 +18,14 @@ NT = B // P
 GT = 4
 NG = NT // GT
 W = D // 2
+LA = 6
 
 FLOPS = 2 * B * NP * D
 
 TINY = 2.0 ** -116
 SQRT_TINY = 2.0 ** -58
 
-BATCHES = [(0, 32), (32, 32), (64, 32), (96, 24), (120, 8)]
+BATCHES = [(0, 32), (32, 32), (64, 32), (96, 28), (124, 4)]
 
 
 def tile_lvq_t_kernel(tc, x, prototypes, out):
@@ -37,78 +38,55 @@ def tile_lvq_t_kernel(tc, x, prototypes, out):
         xpool = ctx.enter_context(tc.tile_pool(name="xpool", bufs=8))
         work = ctx.enter_context(tc.tile_pool(name="work", bufs=3))
         fin = ctx.enter_context(tc.tile_pool(name="fin", bufs=2))
-        pxt = ctx.enter_context(tc.psum_pool(name="pxt", bufs=5))
+        pxt = ctx.enter_context(tc.psum_pool(name="pxt", bufs=6))
         pacc = ctx.enter_context(tc.psum_pool(name="pacc", bufs=2))
-        pset = ctx.enter_context(tc.psum_pool(name="pset", bufs=1))
+        ctx.enter_context(tc.manual_schedule())
 
-        warm = const.tile([P, 1], F32, name="warm")
-        nc.vector.memset(warm[:], 1.0)
-        warm2 = const.tile([P, 1], F32, name="warm2")
-        nc.scalar.activation(out=warm2[:], in_=warm[:], func=ACT.Sqrt)
+        xs_of, xt_of, grp_of, mx_of, acc_of, tt_of, fin_of = {}, {}, {}, {}, {}, {}, {}
 
-        ident = const.tile([P, P], F32, name="ident")
-        make_identity(nc, ident[:])
-        ones = const.tile([P, P], F32, name="ones")
-        nc.vector.memset(ones[:], 1.0)
-
-        x2 = const.tile([P, NT], F32, name="x2")
-        mn = const.tile([P, NT * NC], F32, name="mn")
+        def load(g, pieces):
+            xs = xpool.tile([P, GT * D], BF16, name="xs", tag="xs")
+            xs_of[g] = xs
+            for (c0, c1) in pieces:
+                nc.sync.dma_start(out=xs[:, c0:c1], in_=xv[:, g * GT * D + c0:g * GT * D + c1])
 
         def transpose_words(src32, dst):
             for q in range(4):
                 nc.tensor.transpose(dst[:, q * P:(q + 1) * P], src32[:, q * P:(q + 1) * P], ident[:])
 
-        def evacuate(eng_copy, dst32, src):
-            eng_copy(
+        def evacuate(dst32, src):
+            nc.vector.tensor_copy(
                 out=dst32.rearrange("p (g b u) -> p g b u", g=2, u=2),
                 in_=src.rearrange("p (g u b) -> p g b u", g=2, u=2),
             )
 
-        pr = const.tile([P, D], BF16, name="pr")
-        nc.sync.dma_start(out=pr[:], in_=prototypes)
-        pjunk = const.tile([P, D], BF16, name="pjunk")
-        p2 = const.tile([P, 1], F32, name="p2")
-        nc.scalar.activation(out=pjunk[:], in_=pr[:], func=ACT.Square, accum_out=p2[:])
-        p2rep = const.tile([P, P], F32, name="p2rep")
-        nc.vector.tensor_scalar_mul(out=p2rep[:], in0=ones[:], scalar1=p2[:, 0:1])
-        p2t = pset.tile([P, P], F32, name="p2t")
-        nc.tensor.transpose(p2t[:], p2rep[:], ident[:])
-        p2b = const.tile([P, P], F32, name="p2b")
-        nc.vector.tensor_copy(out=p2b[:], in_=p2t[:])
+        def t_x(g, j):
+            xt = pxt.tile([P, W], F32, name="xt", tag="xt")
+            xt_of[(g, j)] = xt
+            transpose_words(xs_of[g][:].bitcast(F32)[:, j * W:(j + 1) * W], xt)
 
-        pxtile = pxt.tile([P, W], F32, name="xt", tag="xt")
-        transpose_words(pr[:].bitcast(F32), pxtile)
-        pgrp = const.tile([P, D], BF16, name="pgrp", align_bytes=64)
-        evacuate(nc.vector.tensor_copy, pgrp[:].bitcast(F32), pxtile[:])
-        pcodes = const.tile([P, D // 4], U32, name="pcodes", align_bytes=64)
-        pscl = const.tile([P, D // 4], U8, name="pscl", align_bytes=64)
-        nc.vector.quantize_mx(out=pcodes[:].bitcast(FP8X4), scales=pscl[:], in_=pgrp[:])
+        def e_x(g, j):
+            if j == 0:
+                grp_of[g] = work.tile([P, GT * D], BF16, name="grp", tag="grp", align_bytes=64)
+            evacuate(grp_of[g][:].bitcast(F32)[:, j * W:(j + 1) * W], xt_of[(g, j)][:])
 
-        state = {}
+        def sq_x(g, j):
+            t = g * GT + j
+            junk = work.tile([P, D], BF16, name="junk", tag="junk")
+            nc.scalar.activation(
+                out=junk[:], in_=xs_of[g][:, j * D:(j + 1) * D], func=ACT.Square, accum_out=x2[:, t:t + 1]
+            )
 
-        def stage_a(g):
-            xs = xpool.tile([P, GT * D], BF16, name="xs", tag="xs")
-            nc.sync.dma_start(out=xs[:], in_=xv[:, g * GT * D:(g + 1) * GT * D])
-            xs32 = xs[:].bitcast(F32)
-            grp = work.tile([P, GT * D], BF16, name="grp", tag="grp", align_bytes=64)
-            grp32 = grp[:].bitcast(F32)
-            for j in range(GT):
-                t = g * GT + j
-                junk = work.tile([P, D], BF16, name="junk", tag="junk")
-                nc.scalar.activation(
-                    out=junk[:], in_=xs[:, j * D:(j + 1) * D], func=ACT.Square, accum_out=x2[:, t:t + 1]
-                )
-                xt = pxt.tile([P, W], F32, name="xt", tag="xt")
-                transpose_words(xs32[:, j * W:(j + 1) * W], xt)
-                evacuate(nc.vector.tensor_copy, grp32[:, j * W:(j + 1) * W], xt[:])
-            state[g] = grp
-
-        def stage_b(g):
-            grp = state[g]
+        def q_x(g):
             codes = work.tile([P, GT * D // 4], U32, name="codes", tag="codes", align_bytes=64)
             scl = work.tile([P, GT * D // 4], U8, name="scl", tag="scl", align_bytes=64)
-            nc.vector.quantize_mx(out=codes[:].bitcast(FP8X4), scales=scl[:], in_=grp[:])
+            mx_of[g] = (codes, scl)
+            nc.vector.quantize_mx(out=codes[:].bitcast(FP8X4), scales=scl[:], in_=grp_of[g][:])
+
+        def mx_x(g):
+            codes, scl = mx_of[g]
             acc = pacc.tile([P, GT * NP], F32, name="acc", tag="acc")
+            acc_of[g] = acc
             for j in range(GT):
                 for h in range(2):
                     c0 = (j * 2 + h) * P
@@ -121,23 +99,28 @@ def tile_lvq_t_kernel(tc, x, prototypes, out):
                         start=(h == 0),
                         stop=(h == 1),
                     )
+
+        def stt_x(g):
             tt = work.tile([P, GT * NP], F32, name="tt", tag="tt")
+            tt_of[g] = tt
             nc.vector.scalar_tensor_tensor(
                 out=tt[:].rearrange("p (j n) -> p j n", j=GT),
-                in0=acc[:].rearrange("p (j n) -> p j n", j=GT),
+                in0=acc_of[g][:].rearrange("p (j n) -> p j n", j=GT),
                 scalar=-2.0,
                 in1=p2b[:].unsqueeze(1).to_broadcast([P, GT, NP]),
                 op0=ALU.mult,
                 op1=ALU.add,
             )
+
+        def red_x(g):
             nc.vector.tensor_reduce(
                 out=mn[:, g * GT * NC:(g + 1) * GT * NC],
-                in_=tt[:].rearrange("p (m q) -> p m q", q=PPC),
+                in_=tt_of[g][:].rearrange("p (m q) -> p m q", q=PPC),
                 axis=AX.X,
                 op=ALU.min,
             )
 
-        def finish(t0, n):
+        def fin_ab(t0, n):
             s = fin.tile([P, n * NC], F32, name="s", tag="s")
             nc.vector.tensor_tensor(
                 out=s[:].rearrange("p (t c) -> p t c", c=NC),
@@ -146,19 +129,95 @@ def tile_lvq_t_kernel(tc, x, prototypes, out):
                 op=ALU.add,
             )
             nc.vector.tensor_scalar_max(out=s[:], in0=s[:], scalar1=TINY)
+            fin_of[t0] = s
+
+        def fin_c(t0, n):
             r = fin.tile([P, n * NC], F32, name="r", tag="r")
-            nc.scalar.activation(out=r[:], in_=s[:], func=ACT.Sqrt)
+            nc.scalar.activation(out=r[:], in_=fin_of[t0][:], func=ACT.Sqrt)
+            fin_of[t0] = r
+
+        def fin_d(t0, n):
             res = fin.tile([P, n * NC], F32, name="res", tag="res")
             nc.vector.tensor_scalar(
-                out=res[:], in0=r[:], scalar1=SQRT_TINY, scalar2=-1.0, op0=ALU.subtract, op1=ALU.mult
+                out=res[:], in0=fin_of[t0][:], scalar1=SQRT_TINY, scalar2=-1.0, op0=ALU.subtract, op1=ALU.mult
             )
             nc.sync.dma_start(out=outv[:, t0 * NC:(t0 + n) * NC], in_=res[:])
 
-        ends = dict(((t0 + n) // GT - 1, (t0, n)) for (t0, n) in BATCHES)
+        load(0, [(0, D)])
+        pr = const.tile([P, D], BF16, name="pr")
+        nc.sync.dma_start(out=pr[:], in_=prototypes)
+        xs0 = xs_of[0]
+        nc.sync.dma_start(out=xs0[:, D:GT * D], in_=xv[:, D:GT * D])
+        for g in range(1, LA):
+            load(g, [(0, GT * D)])
+
+        warm = const.tile([P, 1], F32, name="warm")
+        nc.vector.memset(warm[:], 1.0)
+        warm2 = const.tile([P, 1], F32, name="warm2")
+        nc.scalar.activation(out=warm2[:], in_=warm[:], func=ACT.Sqrt)
+        ident = const.tile([P, P], F32, name="ident")
+        make_identity(nc, ident[:])
+        ones = const.tile([P, P], F32, name="ones")
+        nc.vector.memset(ones[:], 1.0)
+        x2 = const.tile([P, NT], F32, name="x2")
+        mn = const.tile([P, NT * NC], F32, name="mn")
+        pjunk = const.tile([P, D], BF16, name="pjunk")
+        p2 = const.tile([P, 1], F32, name="p2")
+        p2rep = const.tile([P, P], F32, name="p2rep")
+        p2b = const.tile([P, P], F32, name="p2b")
+        pgrp = const.tile([P, D], BF16, name="pgrp", align_bytes=64)
+        pcodes = const.tile([P, D // 4], U32, name="pcodes", align_bytes=64)
+        pscl = const.tile([P, D // 4], U8, name="pscl", align_bytes=64)
+
+        t_x(0, 0)
+        pxtile = pxt.tile([P, W], F32, name="xt", tag="xt")
+        transpose_words(pr[:].bitcast(F32), pxtile)
+        t_x(0, 1)
+        t_x(0, 2)
+        t_x(0, 3)
+
+        ab_at = dict(((t0 + n) // GT + 1, (t0, n)) for (t0, n) in BATCHES)
+        d_at = dict(((t0 + n) // GT + 2, (t0, n)) for (t0, n) in BATCHES)
+        done_ab, done_d = [], []
+
         for i in range(NG + 1):
+            if i + LA < NG:
+                load(i + LA, [(0, GT * D)])
             if i < NG:
-                stage_a(i)
+                for j in range(GT):
+                    if i + 1 < NG:
+                        t_x(i + 1, j)
+                    e_x(i, j)
+                    sq_x(i, j)
+                    if i == 0 and j == 0:
+                        nc.scalar.activation(out=pjunk[:], in_=pr[:], func=ACT.Square, accum_out=p2[:])
+                        evacuate(pgrp[:].bitcast(F32), pxtile[:])
+            if i in d_at:
+                fin_d(*d_at[i])
+                done_d.append(d_at[i])
+            if i in ab_at:
+                fin_ab(*ab_at[i])
+                fin_c(*ab_at[i])
+                done_ab.append(ab_at[i])
+            if i == 0:
+                nc.vector.quantize_mx(out=pcodes[:].bitcast(FP8X4), scales=pscl[:], in_=pgrp[:])
+                nc.vector.tensor_scalar_mul(out=p2rep[:], in0=ones[:], scalar1=p2[:, 0:1])
+                p2t = pacc.tile([P, P], F32, name="acc", tag="acc")
+                nc.tensor.transpose(p2t[:], p2rep[:], ident[:])
+            if i == 1:
+                nc.vector.tensor_copy(out=p2b[:], in_=p2t[:])
             if i >= 1:
-                stage_b(i - 1)
-                if (i - 1) in ends:
-                    finish(*ends[i - 1])
+                stt_x(i - 1)
+            if i < NG:
+                q_x(i)
+                mx_x(i)
+            if i >= 1:
+                red_x(i - 1)
+
+        for bt in BATCHES:
+            if bt not in done_ab:
+                fin_ab(*bt)
+                fin_c(*bt)
+        for bt in BATCHES:
+            if bt not in done_d:
+                fin_d(*bt)

@@ -26,6 +26,8 @@ TINY = 2.0 ** -116
 SQRT_TINY = 2.0 ** -58
 
 BATCHES = [(0, 32), (32, 32), (64, 32), (96, 28), (124, 4)]
+GRAM = [1, 4, 6, 9, 12, 14, 17, 20, 22, 25, 28, 30]
+S_EVAC = [1, 3, 4, 6, 9, 11, 12, 14, 17, 19, 20, 22, 25, 27, 28, 30]
 
 
 def tile_lvq_t_kernel(tc, x, prototypes, out):
@@ -42,7 +44,7 @@ def tile_lvq_t_kernel(tc, x, prototypes, out):
         pacc = ctx.enter_context(tc.psum_pool(name="pacc", bufs=2))
         ctx.enter_context(tc.manual_schedule())
 
-        xs_of, xt_of, grp_of, mx_of, acc_of, tt_of, fin_of = {}, {}, {}, {}, {}, {}, {}
+        xs_of, xt_of, grp_of, mx_of, acc_of, tt_of, fin_of, gram_of = {}, {}, {}, {}, {}, {}, {}, {}
 
         def load(g, pieces):
             xs = xpool.tile([P, GT * D], BF16, name="xs", tag="xs")
@@ -54,8 +56,8 @@ def tile_lvq_t_kernel(tc, x, prototypes, out):
             for q in range(4):
                 nc.tensor.transpose(dst[:, q * P:(q + 1) * P], src32[:, q * P:(q + 1) * P], ident[:])
 
-        def evacuate(dst32, src):
-            nc.vector.tensor_copy(
+        def evacuate(dst32, src, copy=None):
+            (copy or nc.vector.tensor_copy)(
                 out=dst32.rearrange("p (g b u) -> p g b u", g=2, u=2),
                 in_=src.rearrange("p (g u b) -> p g b u", g=2, u=2),
             )
@@ -66,9 +68,46 @@ def tile_lvq_t_kernel(tc, x, prototypes, out):
             transpose_words(xs_of[g][:].bitcast(F32)[:, j * W:(j + 1) * W], xt)
 
         def e_x(g, j):
-            if j == 0:
+            if g not in grp_of:
                 grp_of[g] = work.tile([P, GT * D], BF16, name="grp", tag="grp", align_bytes=64)
-            evacuate(grp_of[g][:].bitcast(F32)[:, j * W:(j + 1) * W], xt_of[(g, j)][:])
+            on_scalar = j == GT - 1 and g in S_EVAC
+            evacuate(
+                grp_of[g][:].bitcast(F32)[:, j * W:(j + 1) * W],
+                xt_of[(g, j)][:],
+                nc.scalar.copy if on_scalar else None,
+            )
+
+        def gram_x(g):
+            gram = pxt.tile([P, W], F32, name="xt", tag="xt")
+            gram_of[g] = gram
+            gv = grp_of[g][:].rearrange("p (j h b t) -> p j h b t", j=GT, h=2, t=4)
+            for h in range(2):
+                for t in range(4):
+                    nc.tensor.matmul(
+                        out=gram[:, 0:P],
+                        lhsT=gv[:, 0, h, :, t],
+                        rhs=gv[:, 0, h, :, t],
+                        start=(h == 0 and t == 0),
+                        stop=(h == 1 and t == 3),
+                    )
+
+        def diag_x(g):
+            n = GRAM.index(g)
+            gj = work.tile([P, P], F32, name="gj", tag="gj")
+            nc.vector.scalar_tensor_tensor(
+                out=gj[:],
+                in0=gram_of[g][:, 0:P],
+                scalar=1.0,
+                in1=ident[:],
+                op0=ALU.mult,
+                op1=ALU.mult,
+                accum_out=x2g[:, n:n + 1],
+            )
+
+        def add_x(g):
+            n = GRAM.index(g)
+            c0 = g * GT * NC
+            nc.vector.tensor_scalar_add(out=mn[:, c0:c0 + NC], in0=mn[:, c0:c0 + NC], scalar1=x2g[:, n:n + 1])
 
         def sq_x(g, j):
             t = g * GT + j
@@ -160,6 +199,8 @@ def tile_lvq_t_kernel(tc, x, prototypes, out):
         ones = const.tile([P, P], F32, name="ones")
         nc.vector.memset(ones[:], 1.0)
         x2 = const.tile([P, NT], F32, name="x2")
+        nc.vector.memset(x2[:], 0.0)
+        x2g = const.tile([P, len(GRAM)], F32, name="x2g")
         mn = const.tile([P, NT * NC], F32, name="mn")
         pjunk = const.tile([P, D], BF16, name="pjunk")
         p2 = const.tile([P, 1], F32, name="p2")
@@ -177,27 +218,37 @@ def tile_lvq_t_kernel(tc, x, prototypes, out):
         t_x(0, 3)
 
         ab_at = dict(((t0 + n) // GT + 1, (t0, n)) for (t0, n) in BATCHES)
-        d_at = dict(((t0 + n) // GT + 2, (t0, n)) for (t0, n) in BATCHES)
-        done_ab, done_d = [], []
+        c_at = dict(((t0 + n) // GT + 2, (t0, n)) for (t0, n) in BATCHES)
+        d_at = dict(((t0 + n) // GT + 3, (t0, n)) for (t0, n) in BATCHES)
+        done_ab, done_c, done_d = [], [], []
 
         for i in range(NG + 1):
             if i + LA < NG:
                 load(i + LA, [(0, GT * D)])
             if i < NG:
-                for j in range(GT):
+                if i in c_at:
+                    fin_c(*c_at[i])
+                    done_c.append(c_at[i])
+                order = [GT - 1, 0, 1, 2] if i in S_EVAC else [0, 1, 2, 3]
+                for j in order:
                     if i + 1 < NG:
-                        t_x(i + 1, j)
+                        t_x(i + 1, order.index(j))
                     e_x(i, j)
-                    sq_x(i, j)
+                for j in range(GT):
+                    if j > 0 or i not in GRAM:
+                        sq_x(i, j)
                     if i == 0 and j == 0:
                         nc.scalar.activation(out=pjunk[:], in_=pr[:], func=ACT.Square, accum_out=p2[:])
                         evacuate(pgrp[:].bitcast(F32), pxtile[:])
+            if i - 1 in GRAM:
+                diag_x(i - 1)
+            if i - 2 in GRAM:
+                add_x(i - 2)
             if i in d_at:
                 fin_d(*d_at[i])
                 done_d.append(d_at[i])
             if i in ab_at:
                 fin_ab(*ab_at[i])
-                fin_c(*ab_at[i])
                 done_ab.append(ab_at[i])
             if i == 0:
                 nc.vector.quantize_mx(out=pcodes[:].bitcast(FP8X4), scales=pscl[:], in_=pgrp[:])
@@ -210,6 +261,8 @@ def tile_lvq_t_kernel(tc, x, prototypes, out):
                 stt_x(i - 1)
             if i < NG:
                 q_x(i)
+                if i in GRAM:
+                    gram_x(i)
                 mx_x(i)
             if i >= 1:
                 red_x(i - 1)
@@ -217,6 +270,7 @@ def tile_lvq_t_kernel(tc, x, prototypes, out):
         for bt in BATCHES:
             if bt not in done_ab:
                 fin_ab(*bt)
+            if bt not in done_c:
                 fin_c(*bt)
         for bt in BATCHES:
             if bt not in done_d:

@@ -25,9 +25,10 @@ FLOPS = 2 * B * NP * D
 TINY = 2.0 ** -116
 SQRT_TINY = 2.0 ** -58
 
-BATCHES = [(0, 32), (32, 32), (64, 32), (96, 28), (124, 4)]
-GRAM = [1, 4, 6, 9, 12, 14, 17, 20, 22, 25, 28, 30]
-S_EVAC = [1, 3, 4, 6, 9, 11, 12, 14, 17, 19, 20, 22, 25, 27, 28, 30]
+BATCHES = [(0, 32, 10), (32, 32, 18), (64, 32, 26), (96, 28, 32), (124, 4, 33)]
+GRAM = [1, 3, 5, 9, 11, 13, 17, 19, 21, 25, 27, 29]
+GSQ = [0, 2, 4, 6, 8, 10, 12, 14, 16, 18, 20, 22, 24, 26, 28]
+S_TWO = [1, 5, 9, 13, 17, 21, 25, 29]
 
 
 def tile_lvq_t_kernel(tc, x, prototypes, out):
@@ -44,20 +45,28 @@ def tile_lvq_t_kernel(tc, x, prototypes, out):
         pacc = ctx.enter_context(tc.psum_pool(name="pacc", bufs=2))
         ctx.enter_context(tc.manual_schedule())
 
-        xs_of, xt_of, grp_of, mx_of, acc_of, tt_of, fin_of, gram_of = {}, {}, {}, {}, {}, {}, {}, {}
+        xs_of, xt_of, grp_of, mx_of, acc_of, tt_of, fin_of, gram_of, gsq_of = {}, {}, {}, {}, {}, {}, {}, {}, {}
 
-        def load(g, pieces):
-            xs = xpool.tile([P, GT * D], BF16, name="xs", tag="xs")
-            xs_of[g] = xs
-            for (c0, c1) in pieces:
-                nc.sync.dma_start(out=xs[:, c0:c1], in_=xv[:, g * GT * D + c0:g * GT * D + c1])
+        def scalar_banks(g):
+            if g == 0:
+                return []
+            if g in S_TWO:
+                return [3, 2]
+            if g in GRAM or g in GSQ:
+                return [3]
+            return []
+
+        def load(g, c0, c1):
+            if g not in xs_of:
+                xs_of[g] = xpool.tile([P, GT * D], BF16, name="xs", tag="xs")
+            nc.sync.dma_start(out=xs_of[g][:, c0:c1], in_=xv[:, g * GT * D + c0:g * GT * D + c1])
 
         def transpose_words(src32, dst):
             for q in range(4):
                 nc.tensor.transpose(dst[:, q * P:(q + 1) * P], src32[:, q * P:(q + 1) * P], ident[:])
 
-        def evacuate(dst32, src, copy=None):
-            (copy or nc.vector.tensor_copy)(
+        def evacuate(copy, dst32, src):
+            copy(
                 out=dst32.rearrange("p (g b u) -> p g b u", g=2, u=2),
                 in_=src.rearrange("p (g u b) -> p g b u", g=2, u=2),
             )
@@ -70,44 +79,11 @@ def tile_lvq_t_kernel(tc, x, prototypes, out):
         def e_x(g, j):
             if g not in grp_of:
                 grp_of[g] = work.tile([P, GT * D], BF16, name="grp", tag="grp", align_bytes=64)
-            on_scalar = j == GT - 1 and g in S_EVAC
             evacuate(
+                nc.scalar.copy if j in scalar_banks(g) else nc.vector.tensor_copy,
                 grp_of[g][:].bitcast(F32)[:, j * W:(j + 1) * W],
                 xt_of[(g, j)][:],
-                nc.scalar.copy if on_scalar else None,
             )
-
-        def gram_x(g):
-            gram = pxt.tile([P, W], F32, name="xt", tag="xt")
-            gram_of[g] = gram
-            gv = grp_of[g][:].rearrange("p (j h b t) -> p j h b t", j=GT, h=2, t=4)
-            for h in range(2):
-                for t in range(4):
-                    nc.tensor.matmul(
-                        out=gram[:, 0:P],
-                        lhsT=gv[:, 0, h, :, t],
-                        rhs=gv[:, 0, h, :, t],
-                        start=(h == 0 and t == 0),
-                        stop=(h == 1 and t == 3),
-                    )
-
-        def diag_x(g):
-            n = GRAM.index(g)
-            gj = work.tile([P, P], F32, name="gj", tag="gj")
-            nc.vector.scalar_tensor_tensor(
-                out=gj[:],
-                in0=gram_of[g][:, 0:P],
-                scalar=1.0,
-                in1=ident[:],
-                op0=ALU.mult,
-                op1=ALU.mult,
-                accum_out=x2g[:, n:n + 1],
-            )
-
-        def add_x(g):
-            n = GRAM.index(g)
-            c0 = g * GT * NC
-            nc.vector.tensor_scalar_add(out=mn[:, c0:c0 + NC], in0=mn[:, c0:c0 + NC], scalar1=x2g[:, n:n + 1])
 
         def sq_x(g, j):
             t = g * GT + j
@@ -159,6 +135,56 @@ def tile_lvq_t_kernel(tc, x, prototypes, out):
                 op=ALU.min,
             )
 
+        def gram_x(g):
+            gram = pxt.tile([P, W], F32, name="xt", tag="xt")
+            gram_of[g] = gram
+            gv = grp_of[g][:].rearrange("p (j h b t) -> p j h b t", j=GT, h=2, t=4)
+            for h in range(2):
+                for t in range(4):
+                    nc.tensor.matmul(
+                        out=gram[:, 0:P],
+                        lhsT=gv[:, 0, h, :, t],
+                        rhs=gv[:, 0, h, :, t],
+                        start=(h == 0 and t == 0),
+                        stop=(h == 1 and t == 3),
+                    )
+
+        def diag_x(g):
+            n = GRAM.index(g)
+            gj = work.tile([P, P], F32, name="gj", tag="gj")
+            nc.vector.scalar_tensor_tensor(
+                out=gj[:],
+                in0=gram_of[g][:, 0:P],
+                scalar=1.0,
+                in1=ident[:],
+                op0=ALU.mult,
+                op1=ALU.mult,
+                accum_out=x2g[:, n:n + 1],
+            )
+
+        def add_x(t, col):
+            nc.vector.tensor_scalar_add(
+                out=mn[:, t * NC:(t + 1) * NC], in0=mn[:, t * NC:(t + 1) * NC], scalar1=col
+            )
+
+        def gate(g):
+            gg = work.tile([P, 1], F32, name="gg", tag="gg")
+            nc.gpsimd.tensor_copy(out=gg[:], in_=mx_of[g][0][:, 0:1].bitcast(F32))
+
+        def gsq_mul(g):
+            gsq = work.tile([P, D], F32, name="gsq", tag="gsq")
+            gsq_of[g] = gsq
+            nc.gpsimd.tensor_tensor(out=gsq[:], in0=xs_of[g][:, D:2 * D], in1=xs_of[g][:, D:2 * D], op=ALU.mult)
+
+        def gsq_fold(g):
+            gsq = gsq_of[g]
+            for n in (512, 256, 128):
+                nc.gpsimd.tensor_tensor(out=gsq[:, 0:n], in0=gsq[:, 0:n], in1=gsq[:, n:2 * n], op=ALU.add)
+
+        def gsq_red(g):
+            n = GSQ.index(g)
+            nc.vector.tensor_reduce(out=x2h[:, n:n + 1], in_=gsq_of[g][:, 0:P], axis=AX.X, op=ALU.add)
+
         def fin_ab(t0, n):
             s = fin.tile([P, n * NC], F32, name="s", tag="s")
             nc.vector.tensor_tensor(
@@ -182,13 +208,12 @@ def tile_lvq_t_kernel(tc, x, prototypes, out):
             )
             nc.sync.dma_start(out=outv[:, t0 * NC:(t0 + n) * NC], in_=res[:])
 
-        load(0, [(0, D)])
+        load(0, 0, D)
         pr = const.tile([P, D], BF16, name="pr")
         nc.sync.dma_start(out=pr[:], in_=prototypes)
-        xs0 = xs_of[0]
-        nc.sync.dma_start(out=xs0[:, D:GT * D], in_=xv[:, D:GT * D])
+        load(0, D, GT * D)
         for g in range(1, LA):
-            load(g, [(0, GT * D)])
+            load(g, 0, GT * D)
 
         warm = const.tile([P, 1], F32, name="warm")
         nc.vector.memset(warm[:], 1.0)
@@ -201,6 +226,7 @@ def tile_lvq_t_kernel(tc, x, prototypes, out):
         x2 = const.tile([P, NT], F32, name="x2")
         nc.vector.memset(x2[:], 0.0)
         x2g = const.tile([P, len(GRAM)], F32, name="x2g")
+        x2h = const.tile([P, len(GSQ)], F32, name="x2h")
         mn = const.tile([P, NT * NC], F32, name="mn")
         pjunk = const.tile([P, D], BF16, name="pjunk")
         p2 = const.tile([P, 1], F32, name="p2")
@@ -217,36 +243,36 @@ def tile_lvq_t_kernel(tc, x, prototypes, out):
         t_x(0, 2)
         t_x(0, 3)
 
-        ab_at = dict(((t0 + n) // GT + 1, (t0, n)) for (t0, n) in BATCHES)
-        c_at = dict(((t0 + n) // GT + 2, (t0, n)) for (t0, n) in BATCHES)
-        d_at = dict(((t0 + n) // GT + 3, (t0, n)) for (t0, n) in BATCHES)
+        ab_at = dict((it, (t0, n)) for (t0, n, it) in BATCHES)
         done_ab, done_c, done_d = [], [], []
 
         for i in range(NG + 1):
             if i + LA < NG:
-                load(i + LA, [(0, GT * D)])
+                load(i + LA, 0, GT * D)
+            if i - 1 in ab_at and i < NG:
+                fin_c(*ab_at[i - 1])
+                done_c.append(ab_at[i - 1])
             if i < NG:
-                if i in c_at:
-                    fin_c(*c_at[i])
-                    done_c.append(c_at[i])
-                order = [GT - 1, 0, 1, 2] if i in S_EVAC else [0, 1, 2, 3]
-                for j in order:
+                sb = scalar_banks(i)
+                order = sb + [j for j in range(GT) if j not in sb]
+                for k in range(GT):
                     if i + 1 < NG:
-                        t_x(i + 1, order.index(j))
-                    e_x(i, j)
+                        t_x(i + 1, k)
+                    e_x(i, order[k])
+                    if i == 0 and k == 0:
+                        evacuate(nc.vector.tensor_copy, pgrp[:].bitcast(F32), pxtile[:])
                 for j in range(GT):
-                    if j > 0 or i not in GRAM:
+                    if not ((j == 0 and i in GRAM) or (j == 1 and i in GSQ)):
                         sq_x(i, j)
                     if i == 0 and j == 0:
                         nc.scalar.activation(out=pjunk[:], in_=pr[:], func=ACT.Square, accum_out=p2[:])
-                        evacuate(pgrp[:].bitcast(F32), pxtile[:])
-            if i - 1 in GRAM:
-                diag_x(i - 1)
             if i - 2 in GRAM:
-                add_x(i - 2)
-            if i in d_at:
-                fin_d(*d_at[i])
-                done_d.append(d_at[i])
+                add_x((i - 2) * GT, x2g[:, GRAM.index(i - 2):GRAM.index(i - 2) + 1])
+            if i - 3 in GSQ:
+                gsq_red(i - 3)
+            if i - 2 in ab_at and ab_at[i - 2] in done_c:
+                fin_d(*ab_at[i - 2])
+                done_d.append(ab_at[i - 2])
             if i in ab_at:
                 fin_ab(*ab_at[i])
                 done_ab.append(ab_at[i])
@@ -261,17 +287,28 @@ def tile_lvq_t_kernel(tc, x, prototypes, out):
                 stt_x(i - 1)
             if i < NG:
                 q_x(i)
+                mx_x(i)
                 if i in GRAM:
                     gram_x(i)
-                mx_x(i)
+                if i in GSQ:
+                    gate(i)
+                    gsq_mul(i)
+                if i - 1 in GSQ:
+                    gate(i)
+                    gsq_fold(i - 1)
             if i >= 1:
                 red_x(i - 1)
+            if i - 1 in GRAM:
+                diag_x(i - 1)
+            if i - 3 in GSQ:
+                add_x((i - 3) * GT + 1, x2h[:, GSQ.index(i - 3):GSQ.index(i - 3) + 1])
 
-        for bt in BATCHES:
+        rest = [(t0, n) for (t0, n, it) in BATCHES]
+        for bt in rest:
             if bt not in done_ab:
                 fin_ab(*bt)
             if bt not in done_c:
                 fin_c(*bt)
-        for bt in BATCHES:
+        for bt in rest:
             if bt not in done_d:
                 fin_d(*bt)

@@ -17,18 +17,20 @@ P = 128
 NT = B // P
 GT = 4
 NG = NT // GT
+NK = NG // 2
 W = D // 2
 LA = 6
+XT = 5
 
 FLOPS = 2 * B * NP * D
 
 TINY = 2.0 ** -116
 SQRT_TINY = 2.0 ** -58
 
-BATCHES = [(0, 32, 10), (32, 32, 18), (64, 32, 26), (96, 28, 32), (124, 4, 33)]
-GRAM = [1, 3, 5, 9, 11, 13, 17, 19, 21, 25, 27, 29]
-GSQ = [0, 2, 4, 6, 8, 10, 12, 14, 16, 18, 20, 22, 24, 26, 28]
-S_TWO = [1, 5, 9, 13, 17, 21, 25, 29]
+BATCHES = [(0, 32, 5), (32, 32, 9), (64, 32, 13), (96, 24, 16), (120, 8, 17)]
+GRAM_PAIRS = [0, 1, 2, 4, 5, 6, 8, 9, 10, 12, 13, 14]
+S_TWO = [5, 13, 21, 25, 27, 29]
+GSQ_PAIRS = [0, 1, 2, 3, 4, 5, 6, 7, 8, 9, 10, 11, 12, 13, 14]
 
 
 def tile_lvq_t_kernel(tc, x, prototypes, out):
@@ -39,22 +41,21 @@ def tile_lvq_t_kernel(tc, x, prototypes, out):
     with ExitStack() as ctx:
         const = ctx.enter_context(tc.tile_pool(name="const", bufs=1))
         xpool = ctx.enter_context(tc.tile_pool(name="xpool", bufs=8))
-        work = ctx.enter_context(tc.tile_pool(name="work", bufs=3))
+        work = ctx.enter_context(tc.tile_pool(name="work", bufs=4))
+        gpool = ctx.enter_context(tc.tile_pool(name="gpool", bufs=2))
         fin = ctx.enter_context(tc.tile_pool(name="fin", bufs=2))
-        pxt = ctx.enter_context(tc.psum_pool(name="pxt", bufs=6))
+        pxt = ctx.enter_context(tc.psum_pool(name="pxt", bufs=XT))
+        pgram = ctx.enter_context(tc.psum_pool(name="pgram", bufs=1))
         pacc = ctx.enter_context(tc.psum_pool(name="pacc", bufs=2))
         ctx.enter_context(tc.manual_schedule())
 
         xs_of, xt_of, grp_of, mx_of, acc_of, tt_of, fin_of, gram_of, gsq_of = {}, {}, {}, {}, {}, {}, {}, {}, {}
+        stream = {"live": 0, "next": 0}
 
         def scalar_banks(g):
             if g == 0:
                 return []
-            if g in S_TWO:
-                return [3, 2]
-            if g in GRAM or g in GSQ:
-                return [3]
-            return []
+            return [3, 2] if g in S_TWO else [3]
 
         def load(g, c0, c1):
             if g not in xs_of:
@@ -71,10 +72,14 @@ def tile_lvq_t_kernel(tc, x, prototypes, out):
                 in_=src.rearrange("p (g u b) -> p g b u", g=2, u=2),
             )
 
-        def t_x(g, j):
-            xt = pxt.tile([P, W], F32, name="xt", tag="xt")
-            xt_of[(g, j)] = xt
-            transpose_words(xs_of[g][:].bitcast(F32)[:, j * W:(j + 1) * W], xt)
+        def pump():
+            while stream["next"] < NT and stream["live"] < XT:
+                t = stream["next"]
+                xt = pxt.tile([P, W], F32, name="xt", tag="xt")
+                xt_of[t] = xt
+                transpose_words(xs_of[t // GT][:].bitcast(F32)[:, (t % GT) * W:(t % GT + 1) * W], xt)
+                stream["next"] = t + 1
+                stream["live"] = stream["live"] + 1
 
         def e_x(g, j):
             if g not in grp_of:
@@ -82,14 +87,16 @@ def tile_lvq_t_kernel(tc, x, prototypes, out):
             evacuate(
                 nc.scalar.copy if j in scalar_banks(g) else nc.vector.tensor_copy,
                 grp_of[g][:].bitcast(F32)[:, j * W:(j + 1) * W],
-                xt_of[(g, j)][:],
+                xt_of[g * GT + j][:],
             )
+            stream["live"] = stream["live"] - 1
+            pump()
 
         def sq_x(g, j):
             t = g * GT + j
             junk = work.tile([P, D], BF16, name="junk", tag="junk")
             nc.scalar.activation(
-                out=junk[:], in_=xs_of[g][:, j * D:(j + 1) * D], func=ACT.Square, accum_out=x2[:, t:t + 1]
+                out=junk[:], in_=xs_of[g][:, j * D:(j + 1) * D], func=ACT.Square, accum_out=x2s[:, t:t + 1]
             )
 
         def q_x(g):
@@ -136,13 +143,13 @@ def tile_lvq_t_kernel(tc, x, prototypes, out):
             )
 
         def gram_x(g):
-            gram = pxt.tile([P, W], F32, name="xt", tag="xt")
+            gram = pgram.tile([P, P], F32, name="gram", tag="gram")
             gram_of[g] = gram
             gv = grp_of[g][:].rearrange("p (j h b t) -> p j h b t", j=GT, h=2, t=4)
             for h in range(2):
                 for t in range(4):
                     nc.tensor.matmul(
-                        out=gram[:, 0:P],
+                        out=gram[:],
                         lhsT=gv[:, 0, h, :, t],
                         rhs=gv[:, 0, h, :, t],
                         start=(h == 0 and t == 0),
@@ -150,51 +157,48 @@ def tile_lvq_t_kernel(tc, x, prototypes, out):
                     )
 
         def diag_x(g):
-            n = GRAM.index(g)
+            t = g * GT
             gj = work.tile([P, P], F32, name="gj", tag="gj")
             nc.vector.scalar_tensor_tensor(
                 out=gj[:],
-                in0=gram_of[g][:, 0:P],
+                in0=gram_of[g][:],
                 scalar=1.0,
                 in1=ident[:],
                 op0=ALU.mult,
                 op1=ALU.mult,
-                accum_out=x2g[:, n:n + 1],
+                accum_out=x2v[:, t:t + 1],
             )
 
-        def add_x(t, col):
-            nc.vector.tensor_scalar_add(
-                out=mn[:, t * NC:(t + 1) * NC], in0=mn[:, t * NC:(t + 1) * NC], scalar1=col
-            )
-
-        def gate(g):
-            gg = work.tile([P, 1], F32, name="gg", tag="gg")
-            nc.gpsimd.tensor_copy(out=gg[:], in_=mx_of[g][0][:, 0:1].bitcast(F32))
-
-        def gsq_mul(g):
-            gsq = work.tile([P, D], F32, name="gsq", tag="gsq")
+        def gsq_x(g, gate_g):
+            gg = gpool.tile([P, 1], F32, name="gg", tag="gg")
+            nc.gpsimd.tensor_copy(out=gg[:], in_=mx_of[gate_g][0][:, 0:1].bitcast(F32))
+            gsq = gpool.tile([P, D], F32, name="gsq", tag="gsq")
             gsq_of[g] = gsq
             nc.gpsimd.tensor_tensor(out=gsq[:], in0=xs_of[g][:, D:2 * D], in1=xs_of[g][:, D:2 * D], op=ALU.mult)
-
-        def gsq_fold(g):
-            gsq = gsq_of[g]
             for n in (512, 256, 128):
                 nc.gpsimd.tensor_tensor(out=gsq[:, 0:n], in0=gsq[:, 0:n], in1=gsq[:, n:2 * n], op=ALU.add)
 
         def gsq_red(g):
-            n = GSQ.index(g)
-            nc.vector.tensor_reduce(out=x2h[:, n:n + 1], in_=gsq_of[g][:, 0:P], axis=AX.X, op=ALU.add)
+            t = g * GT + 1
+            nc.vector.tensor_reduce(out=x2v[:, t:t + 1], in_=gsq_of[g][:, 0:P], axis=AX.X, op=ALU.add)
 
-        def fin_ab(t0, n):
+        def fin_a0(t0, n):
+            x2c = fin.tile([P, n], F32, name="x2c", tag="x2c")
+            nc.vector.tensor_tensor(out=x2c[:], in0=x2s[:, t0:t0 + n], in1=x2v[:, t0:t0 + n], op=ALU.add)
+            fin_of[t0] = x2c
+
+        def fin_a1(t0, n):
             s = fin.tile([P, n * NC], F32, name="s", tag="s")
             nc.vector.tensor_tensor(
                 out=s[:].rearrange("p (t c) -> p t c", c=NC),
                 in0=mn[:, t0 * NC:(t0 + n) * NC].rearrange("p (t c) -> p t c", c=NC),
-                in1=x2[:, t0:t0 + n].unsqueeze(2).to_broadcast([P, n, NC]),
+                in1=fin_of[t0][:].unsqueeze(2).to_broadcast([P, n, NC]),
                 op=ALU.add,
             )
-            nc.vector.tensor_scalar_max(out=s[:], in0=s[:], scalar1=TINY)
             fin_of[t0] = s
+
+        def fin_b(t0, n):
+            nc.vector.tensor_scalar_max(out=fin_of[t0][:], in0=fin_of[t0][:], scalar1=TINY)
 
         def fin_c(t0, n):
             r = fin.tile([P, n * NC], F32, name="r", tag="r")
@@ -223,10 +227,10 @@ def tile_lvq_t_kernel(tc, x, prototypes, out):
         make_identity(nc, ident[:])
         ones = const.tile([P, P], F32, name="ones")
         nc.vector.memset(ones[:], 1.0)
-        x2 = const.tile([P, NT], F32, name="x2")
-        nc.vector.memset(x2[:], 0.0)
-        x2g = const.tile([P, len(GRAM)], F32, name="x2g")
-        x2h = const.tile([P, len(GSQ)], F32, name="x2h")
+        x2s = const.tile([P, NT], F32, name="x2s")
+        nc.vector.memset(x2s[:], 0.0)
+        x2v = const.tile([P, NT], F32, name="x2v")
+        nc.vector.memset(x2v[:], 0.0)
         mn = const.tile([P, NT * NC], F32, name="mn")
         pjunk = const.tile([P, D], BF16, name="pjunk")
         p2 = const.tile([P, 1], F32, name="p2")
@@ -236,77 +240,88 @@ def tile_lvq_t_kernel(tc, x, prototypes, out):
         pcodes = const.tile([P, D // 4], U32, name="pcodes", align_bytes=64)
         pscl = const.tile([P, D // 4], U8, name="pscl", align_bytes=64)
 
-        t_x(0, 0)
+        stream["live"] = XT - 1
+        pump()
         pxtile = pxt.tile([P, W], F32, name="xt", tag="xt")
         transpose_words(pr[:].bitcast(F32), pxtile)
-        t_x(0, 1)
-        t_x(0, 2)
-        t_x(0, 3)
+        stream["live"] = 2
+        pump()
 
         ab_at = dict((it, (t0, n)) for (t0, n, it) in BATCHES)
         done_ab, done_c, done_d = [], [], []
 
-        for i in range(NG + 1):
-            if i + LA < NG:
-                load(i + LA, 0, GT * D)
-            if i - 1 in ab_at and i < NG:
-                fin_c(*ab_at[i - 1])
-                done_c.append(ab_at[i - 1])
-            if i < NG:
-                sb = scalar_banks(i)
-                order = sb + [j for j in range(GT) if j not in sb]
-                for k in range(GT):
-                    if i + 1 < NG:
-                        t_x(i + 1, k)
-                    e_x(i, order[k])
-                    if i == 0 and k == 0:
-                        evacuate(nc.vector.tensor_copy, pgrp[:].bitcast(F32), pxtile[:])
-                for j in range(GT):
-                    if not ((j == 0 and i in GRAM) or (j == 1 and i in GSQ)):
-                        sq_x(i, j)
-                    if i == 0 and j == 0:
-                        nc.scalar.activation(out=pjunk[:], in_=pr[:], func=ACT.Square, accum_out=p2[:])
-            if i - 2 in GRAM:
-                add_x((i - 2) * GT, x2g[:, GRAM.index(i - 2):GRAM.index(i - 2) + 1])
-            if i - 3 in GSQ:
-                gsq_red(i - 3)
-            if i - 2 in ab_at and ab_at[i - 2] in done_c:
-                fin_d(*ab_at[i - 2])
-                done_d.append(ab_at[i - 2])
-            if i in ab_at:
-                fin_ab(*ab_at[i])
-                done_ab.append(ab_at[i])
-            if i == 0:
+        for k in range(NK + 1):
+            a, b = 2 * k, 2 * k + 1
+            for g in (a + LA, b + LA):
+                if g < NG:
+                    load(g, 0, GT * D)
+            if k - 1 in ab_at and k < NK:
+                fin_c(*ab_at[k - 1])
+                done_c.append(ab_at[k - 1])
+            if k < NK:
+                for g in (a, b):
+                    sb = scalar_banks(g)
+                    for j in sb + [j for j in range(GT) if j not in sb]:
+                        e_x(g, j)
+                        if g == 0 and j == 0:
+                            evacuate(nc.vector.tensor_copy, pgrp[:].bitcast(F32), pxtile[:])
+                            stream["live"] = stream["live"] - 1
+                            pump()
+                    for j in range(GT):
+                        if not ((g == b and j == 0 and k in GRAM_PAIRS) or (g == a and j == 1 and k in GSQ_PAIRS)):
+                            sq_x(g, j)
+                        if g == 0 and j == 0:
+                            nc.scalar.activation(out=pjunk[:], in_=pr[:], func=ACT.Square, accum_out=p2[:])
+            ports = []
+            if k - 1 in ab_at and ab_at[k - 1] in done_c:
+                ports.append((fin_d, ab_at[k - 1]))
+                done_d.append(ab_at[k - 1])
+            if k in ab_at:
+                ports.extend([(fin_a0, ab_at[k]), (fin_a1, ab_at[k]), (fin_b, ab_at[k])])
+                done_ab.append(ab_at[k])
+            if k - 2 in GSQ_PAIRS:
+                gsq_red(a - 4)
+            if k == NK:
+                for (f, bt) in ports:
+                    f(*bt)
+                ports = []
+            if k >= 1:
+                stt_x(a - 2)
+                stt_x(b - 2)
+            if k - 1 in GRAM_PAIRS:
+                diag_x(b - 2)
+            if k == 0:
                 nc.vector.quantize_mx(out=pcodes[:].bitcast(FP8X4), scales=pscl[:], in_=pgrp[:])
                 nc.vector.tensor_scalar_mul(out=p2rep[:], in0=ones[:], scalar1=p2[:, 0:1])
-                p2t = pacc.tile([P, P], F32, name="acc", tag="acc")
+                p2t = pgram.tile([P, P], F32, name="gram", tag="gram")
                 nc.tensor.transpose(p2t[:], p2rep[:], ident[:])
-            if i == 1:
-                nc.vector.tensor_copy(out=p2b[:], in_=p2t[:])
-            if i >= 1:
-                stt_x(i - 1)
-            if i < NG:
-                q_x(i)
-                mx_x(i)
-                if i in GRAM:
-                    gram_x(i)
-                if i in GSQ:
-                    gate(i)
-                    gsq_mul(i)
-                if i - 1 in GSQ:
-                    gate(i)
-                    gsq_fold(i - 1)
-            if i >= 1:
-                red_x(i - 1)
-            if i - 1 in GRAM:
-                diag_x(i - 1)
-            if i - 3 in GSQ:
-                add_x((i - 3) * GT + 1, x2h[:, GSQ.index(i - 3):GSQ.index(i - 3) + 1])
+            if k < NK:
+                for (f, bt) in ports[0:1]:
+                    f(*bt)
+                q_x(a)
+                for (f, bt) in ports[1:2]:
+                    f(*bt)
+                q_x(b)
+                for (f, bt) in ports[2:]:
+                    f(*bt)
+                if k == 0:
+                    nc.vector.tensor_copy(out=p2b[:], in_=p2t[:])
+                mx_x(a)
+                mx_x(b)
+                if k in GRAM_PAIRS:
+                    gram_x(b)
+                if k in GSQ_PAIRS:
+                    gsq_x(a, b)
+            if k >= 1:
+                red_x(a - 2)
+                red_x(b - 2)
 
         rest = [(t0, n) for (t0, n, it) in BATCHES]
         for bt in rest:
             if bt not in done_ab:
-                fin_ab(*bt)
+                fin_a0(*bt)
+                fin_a1(*bt)
+                fin_b(*bt)
             if bt not in done_c:
                 fin_c(*bt)
         for bt in rest:

@@ -21,15 +21,16 @@ NK = NG // 2
 W = D // 2
 LA = 6
 XT = 5
+GW = 64
 
 FLOPS = 2 * B * NP * D
 
 TINY = 2.0 ** -116
 SQRT_TINY = 2.0 ** -58
 
-BATCHES = [(0, 32, 5), (32, 32, 9), (64, 32, 13), (96, 24, 16), (120, 8, 17)]
+BATCHES = [(0, 32, 5), (32, 32, 9), (64, 32, 13), (96, 16, 15), (112, 16, 17)]
 GRAM_PAIRS = [0, 1, 2, 4, 5, 6, 8, 9, 10, 12, 13, 14]
-S_TWO = [5, 13, 21, 25, 27, 29]
+S_TWO = [13, 21, 25, 29]
 GSQ_PAIRS = [0, 1, 2, 3, 4, 5, 6, 7, 8, 9, 10, 11, 12, 13, 14]
 
 
@@ -175,12 +176,12 @@ def tile_lvq_t_kernel(tc, x, prototypes, out):
             gsq = gpool.tile([P, D], F32, name="gsq", tag="gsq")
             gsq_of[g] = gsq
             nc.gpsimd.tensor_tensor(out=gsq[:], in0=xs_of[g][:, D:2 * D], in1=xs_of[g][:, D:2 * D], op=ALU.mult)
-            for n in (512, 256, 128):
+            for n in (512, 256, 128, GW):
                 nc.gpsimd.tensor_tensor(out=gsq[:, 0:n], in0=gsq[:, 0:n], in1=gsq[:, n:2 * n], op=ALU.add)
 
         def gsq_red(g):
             t = g * GT + 1
-            nc.vector.tensor_reduce(out=x2v[:, t:t + 1], in_=gsq_of[g][:, 0:P], axis=AX.X, op=ALU.add)
+            nc.vector.tensor_reduce(out=x2v[:, t:t + 1], in_=gsq_of[g][:, 0:GW], axis=AX.X, op=ALU.add)
 
         def fin_a0(t0, n):
             x2c = fin.tile([P, n], F32, name="x2c", tag="x2c")
@@ -259,6 +260,12 @@ def tile_lvq_t_kernel(tc, x, prototypes, out):
                 fin_c(*ab_at[k - 1])
                 done_c.append(ab_at[k - 1])
             if k < NK:
+                squares = [
+                    (g, j)
+                    for g in (a, b)
+                    for j in range(GT)
+                    if not ((g == b and j == 0 and k in GRAM_PAIRS) or (g == a and j == 1 and k in GSQ_PAIRS))
+                ]
                 for g in (a, b):
                     sb = scalar_banks(g)
                     for j in sb + [j for j in range(GT) if j not in sb]:
@@ -267,10 +274,9 @@ def tile_lvq_t_kernel(tc, x, prototypes, out):
                             evacuate(nc.vector.tensor_copy, pgrp[:].bitcast(F32), pxtile[:])
                             stream["live"] = stream["live"] - 1
                             pump()
-                    for j in range(GT):
-                        if not ((g == b and j == 0 and k in GRAM_PAIRS) or (g == a and j == 1 and k in GSQ_PAIRS)):
-                            sq_x(g, j)
-                        if g == 0 and j == 0:
+                    for (g2, j2) in (squares[0:2] if g == a else squares[2:]):
+                        sq_x(g2, j2)
+                        if g2 == 0 and j2 == 0:
                             nc.scalar.activation(out=pjunk[:], in_=pr[:], func=ACT.Square, accum_out=p2[:])
             ports = []
             if k - 1 in ab_at and ab_at[k - 1] in done_c:

@@ -21,7 +21,7 @@ NK = NG // 2
 W = D // 2
 LA = 6
 XT = 5
-GW = 64
+GW = 128
 
 FLOPS = 2 * B * NP * D
 
@@ -176,7 +176,7 @@ def tile_lvq_t_kernel(tc, x, prototypes, out):
             gsq = gpool.tile([P, D], F32, name="gsq", tag="gsq")
             gsq_of[g] = gsq
             nc.gpsimd.tensor_tensor(out=gsq[:], in0=xs_of[g][:, D:2 * D], in1=xs_of[g][:, D:2 * D], op=ALU.mult)
-            for n in (512, 256, 128, GW):
+            for n in (512, 256, GW):
                 nc.gpsimd.tensor_tensor(out=gsq[:, 0:n], in0=gsq[:, 0:n], in1=gsq[:, n:2 * n], op=ALU.add)
 
         def gsq_red(g):

@@ -29,9 +29,10 @@ TINY = 2.0 ** -116
 SQRT_TINY = 2.0 ** -58
 
 BATCHES = [(0, 32, 5), (32, 32, 9), (64, 32, 13), (96, 16, 15), (112, 16, 17)]
-GRAM_PAIRS = [0, 1, 2, 4, 5, 6, 8, 9, 10, 12, 13, 14]
-S_TWO = [13, 21, 25, 29]
-GSQ_PAIRS = [0, 1, 2, 3, 4, 5, 6, 7, 8, 9, 10, 11, 12, 13, 14]
+GRAM_PAIRS = [0, 1, 2, 3, 4, 5, 6, 8, 9, 10, 12, 13, 14]
+GRAM_PART = 3
+S_TWO = [13, 21, 29]
+GSQ_PAIRS = range(1, NK)
 
 
 def tile_lvq_t_kernel(tc, x, prototypes, out):
@@ -93,11 +94,11 @@ def tile_lvq_t_kernel(tc, x, prototypes, out):
             stream["live"] = stream["live"] - 1
             pump()
 
-        def sq_x(g, j):
+        def sq_x(g, j, c0=0):
             t = g * GT + j
             junk = work.tile([P, D], BF16, name="junk", tag="junk")
             nc.scalar.activation(
-                out=junk[:], in_=xs_of[g][:, j * D:(j + 1) * D], func=ACT.Square, accum_out=x2s[:, t:t + 1]
+                out=junk[:, c0:D], in_=xs_of[g][:, j * D + c0:(j + 1) * D], func=ACT.Square, accum_out=x2s[:, t:t + 1]
             )
 
         def q_x(g):
@@ -124,10 +125,11 @@ def tile_lvq_t_kernel(tc, x, prototypes, out):
                     )
 
         def stt_x(g):
-            tt = work.tile([P, GT * NP], F32, name="tt", tag="tt")
-            tt_of[g] = tt
+            if g % 2 == 0:
+                tt_of[g // 2] = work.tile([P, 2 * GT * NP], F32, name="tt", tag="tt")
+            c0 = g % 2 * GT * NP
             nc.vector.scalar_tensor_tensor(
-                out=tt[:].rearrange("p (j n) -> p j n", j=GT),
+                out=tt_of[g // 2][:, c0:c0 + GT * NP].rearrange("p (j n) -> p j n", j=GT),
                 in0=acc_of[g][:].rearrange("p (j n) -> p j n", j=GT),
                 scalar=-2.0,
                 in1=p2b[:].unsqueeze(1).to_broadcast([P, GT, NP]),
@@ -135,10 +137,10 @@ def tile_lvq_t_kernel(tc, x, prototypes, out):
                 op1=ALU.add,
             )
 
-        def red_x(g):
+        def red_x(k):
             nc.vector.tensor_reduce(
-                out=mn[:, g * GT * NC:(g + 1) * GT * NC],
-                in_=tt_of[g][:].rearrange("p (m q) -> p m q", q=PPC),
+                out=mn[:, 2 * k * GT * NC:2 * (k + 1) * GT * NC],
+                in_=tt_of[k][:].rearrange("p (m q) -> p m q", q=PPC),
                 axis=AX.X,
                 op=ALU.min,
             )
@@ -147,15 +149,10 @@ def tile_lvq_t_kernel(tc, x, prototypes, out):
             gram = pgram.tile([P, P], F32, name="gram", tag="gram")
             gram_of[g] = gram
             gv = grp_of[g][:].rearrange("p (j h b t) -> p j h b t", j=GT, h=2, t=4)
-            for h in range(2):
-                for t in range(4):
-                    nc.tensor.matmul(
-                        out=gram[:],
-                        lhsT=gv[:, 0, h, :, t],
-                        rhs=gv[:, 0, h, :, t],
-                        start=(h == 0 and t == 0),
-                        stop=(h == 1 and t == 3),
-                    )
+            n = 6 if g // 2 == GRAM_PART else 8
+            for i in range(n):
+                sl = gv[:, 0, i // 4, :, i % 4]
+                nc.tensor.matmul(out=gram[:], lhsT=sl, rhs=sl, start=(i == 0), stop=(i == n - 1))
 
         def diag_x(g):
             t = g * GT
@@ -170,18 +167,19 @@ def tile_lvq_t_kernel(tc, x, prototypes, out):
                 accum_out=x2v[:, t:t + 1],
             )
 
-        def gsq_x(g, gate_g):
+        def gate_x(g):
             gg = gpool.tile([P, 1], F32, name="gg", tag="gg")
-            nc.gpsimd.tensor_copy(out=gg[:], in_=mx_of[gate_g][0][:, 0:1].bitcast(F32))
+            nc.gpsimd.tensor_copy(out=gg[:], in_=mx_of[g][0][:, 0:1].bitcast(F32))
+
+        def gsq_x(key, src):
             gsq = gpool.tile([P, D], F32, name="gsq", tag="gsq")
-            gsq_of[g] = gsq
-            nc.gpsimd.tensor_tensor(out=gsq[:], in0=xs_of[g][:, D:2 * D], in1=xs_of[g][:, D:2 * D], op=ALU.mult)
+            gsq_of[key] = gsq
+            nc.gpsimd.tensor_tensor(out=gsq[:], in0=src, in1=src, op=ALU.mult)
             for n in (512, 256, GW):
                 nc.gpsimd.tensor_tensor(out=gsq[:, 0:n], in0=gsq[:, 0:n], in1=gsq[:, n:2 * n], op=ALU.add)
 
-        def gsq_red(g):
-            t = g * GT + 1
-            nc.vector.tensor_reduce(out=x2v[:, t:t + 1], in_=gsq_of[g][:, 0:GW], axis=AX.X, op=ALU.add)
+        def gsq_red(key, col):
+            nc.vector.tensor_reduce(out=col, in_=gsq_of[key][:, 0:GW], axis=AX.X, op=ALU.add)
 
         def fin_a0(t0, n):
             x2c = fin.tile([P, n], F32, name="x2c", tag="x2c")
@@ -233,13 +231,14 @@ def tile_lvq_t_kernel(tc, x, prototypes, out):
         x2v = const.tile([P, NT], F32, name="x2v")
         nc.vector.memset(x2v[:], 0.0)
         mn = const.tile([P, NT * NC], F32, name="mn")
-        pjunk = const.tile([P, D], BF16, name="pjunk")
         p2 = const.tile([P, 1], F32, name="p2")
         p2rep = const.tile([P, P], F32, name="p2rep")
         p2b = const.tile([P, P], F32, name="p2b")
         pgrp = const.tile([P, D], BF16, name="pgrp", align_bytes=64)
         pcodes = const.tile([P, D // 4], U32, name="pcodes", align_bytes=64)
         pscl = const.tile([P, D // 4], U8, name="pscl", align_bytes=64)
+
+        gsq_x("p", pr[:])
 
         stream["live"] = XT - 1
         pump()
@@ -268,6 +267,10 @@ def tile_lvq_t_kernel(tc, x, prototypes, out):
                 ]
                 for g in (a, b):
                     sb = scalar_banks(g)
+                    if g == 1:
+                        for (g2, j2) in squares[2:5]:
+                            sq_x(g2, j2)
+                        squares = squares[0:2] + squares[5:]
                     for j in sb + [j for j in range(GT) if j not in sb]:
                         e_x(g, j)
                         if g == 0 and j == 0:
@@ -276,8 +279,8 @@ def tile_lvq_t_kernel(tc, x, prototypes, out):
                             pump()
                     for (g2, j2) in (squares[0:2] if g == a else squares[2:]):
                         sq_x(g2, j2)
-                        if g2 == 0 and j2 == 0:
-                            nc.scalar.activation(out=pjunk[:], in_=pr[:], func=ACT.Square, accum_out=p2[:])
+                    if g == b and k == GRAM_PART:
+                        sq_x(b, 0, 768)
             ports = []
             if k - 1 in ab_at and ab_at[k - 1] in done_c:
                 ports.append((fin_d, ab_at[k - 1]))
@@ -285,8 +288,8 @@ def tile_lvq_t_kernel(tc, x, prototypes, out):
             if k in ab_at:
                 ports.extend([(fin_a0, ab_at[k]), (fin_a1, ab_at[k]), (fin_b, ab_at[k])])
                 done_ab.append(ab_at[k])
-            if k - 2 in GSQ_PAIRS:
-                gsq_red(a - 4)
+            if k - 1 in GSQ_PAIRS:
+                gsq_red(a - 2, x2v[:, (a - 2) * GT + 1:(a - 2) * GT + 2])
             if k == NK:
                 for (f, bt) in ports:
                     f(*bt)
@@ -298,6 +301,7 @@ def tile_lvq_t_kernel(tc, x, prototypes, out):
                 diag_x(b - 2)
             if k == 0:
                 nc.vector.quantize_mx(out=pcodes[:].bitcast(FP8X4), scales=pscl[:], in_=pgrp[:])
+                gsq_red("p", p2[:])
                 nc.vector.tensor_scalar_mul(out=p2rep[:], in0=ones[:], scalar1=p2[:, 0:1])
                 p2t = pgram.tile([P, P], F32, name="gram", tag="gram")
                 nc.tensor.transpose(p2t[:], p2rep[:], ident[:])
@@ -316,11 +320,11 @@ def tile_lvq_t_kernel(tc, x, prototypes, out):
                 mx_x(b)
                 if k in GRAM_PAIRS:
                     gram_x(b)
-                if k in GSQ_PAIRS:
-                    gsq_x(a, b)
+                if k + 1 in GSQ_PAIRS:
+                    gate_x(b)
+                    gsq_x(a + 2, xs_of[a + 2][:, D:2 * D])
             if k >= 1:
-                red_x(a - 2)
-                red_x(b - 2)
+                red_x(k - 1)
 
         rest = [(t0, n) for (t0, n, it) in BATCHES]
         for bt in rest:

@@ -31,7 +31,7 @@ SQRT_TINY = 2.0 ** -58
 BATCHES = [(0, 32, 5), (32, 32, 9), (64, 32, 13), (96, 16, 15), (112, 16, 17)]
 GRAM_PAIRS = [0, 1, 2, 3, 4, 5, 6, 8, 9, 10, 12, 13, 14]
 GRAM_PART = 3
-S_TWO = [13, 21, 29]
+S_TWO = range(5, NG, 3)
 GSQ_PAIRS = range(1, NK)
 
 

@@ -267,6 +267,8 @@ def tile_lvq_t_kernel(tc, x, prototypes, out):
                 ]
                 for g in (a, b):
                     sb = scalar_banks(g)
+                    if g == b and k >= 1:
+                        stt_x(a - 2)
                     if g == 1:
                         for (g2, j2) in squares[2:5]:
                             sq_x(g2, j2)
@@ -294,8 +296,9 @@ def tile_lvq_t_kernel(tc, x, prototypes, out):
                 for (f, bt) in ports:
                     f(*bt)
                 ports = []
-            if k >= 1:
+            if k == NK:
                 stt_x(a - 2)
+            if k >= 1:
                 stt_x(b - 2)
             if k - 1 in GRAM_PAIRS:
                 diag_x(b - 2)
@@ -311,15 +314,15 @@ def tile_lvq_t_kernel(tc, x, prototypes, out):
                 q_x(a)
                 for (f, bt) in ports[1:2]:
                     f(*bt)
+                if k == 0:
+                    nc.vector.tensor_copy(out=p2b[:], in_=p2t[:])
                 q_x(b)
                 for (f, bt) in ports[2:]:
                     f(*bt)
-                if k == 0:
-                    nc.vector.tensor_copy(out=p2b[:], in_=p2t[:])
-                mx_x(a)
-                mx_x(b)
                 if k in GRAM_PAIRS:
                     gram_x(b)
+                mx_x(a)
+                mx_x(b)
                 if k + 1 in GSQ_PAIRS:
                     gate_x(b)
                     gsq_x(a + 2, xs_of[a + 2][:, D:2 * D])

@@ -28,10 +28,10 @@ FLOPS = 2 * B * NP * D
 TINY = 2.0 ** -116
 SQRT_TINY = 2.0 ** -58
 
-BATCHES = [(0, 32, 5), (32, 32, 9), (64, 32, 13), (96, 16, 15), (112, 16, 17)]
-GRAM_PAIRS = [0, 1, 2, 3, 4, 5, 6, 8, 9, 10, 12, 13, 14]
+BATCHES = [(0, 48, 7), (48, 48, 13), (96, 16, 15), (112, 16, 17)]
+GRAM_PAIRS = [1, 2, 3, 4, 5, 6, 8, 9, 10, 11, 12, 13, 14]
 GRAM_PART = 3
-S_TWO = range(5, NG, 3)
+S_TWO = list(range(5, NG, 6)) + [30, 31]
 GSQ_PAIRS = range(1, NK)
 
 
@@ -98,7 +98,7 @@ def tile_lvq_t_kernel(tc, x, prototypes, out):
             t = g * GT + j
             junk = work.tile([P, D], BF16, name="junk", tag="junk")
             nc.scalar.activation(
-                out=junk[:, c0:D], in_=xs_of[g][:, j * D + c0:(j + 1) * D], func=ACT.Square, accum_out=x2s[:, t:t + 1]
+                out=junk[:, c0:D], in_=xs_of[g][:, j * D + c0:(j + 1) * D], func=ACT.Square, accum_out=(x2[:, t:t + 1] if c0 == 0 else x2part[:])
             )
 
         def q_x(g):
@@ -164,7 +164,7 @@ def tile_lvq_t_kernel(tc, x, prototypes, out):
                 in1=ident[:],
                 op0=ALU.mult,
                 op1=ALU.mult,
-                accum_out=x2v[:, t:t + 1],
+                accum_out=x2[:, t:t + 1],
             )
 
         def gate_x(g):
@@ -181,17 +181,12 @@ def tile_lvq_t_kernel(tc, x, prototypes, out):
         def gsq_red(key, col):
             nc.vector.tensor_reduce(out=col, in_=gsq_of[key][:, 0:GW], axis=AX.X, op=ALU.add)
 
-        def fin_a0(t0, n):
-            x2c = fin.tile([P, n], F32, name="x2c", tag="x2c")
-            nc.vector.tensor_tensor(out=x2c[:], in0=x2s[:, t0:t0 + n], in1=x2v[:, t0:t0 + n], op=ALU.add)
-            fin_of[t0] = x2c
-
         def fin_a1(t0, n):
             s = fin.tile([P, n * NC], F32, name="s", tag="s")
             nc.vector.tensor_tensor(
                 out=s[:].rearrange("p (t c) -> p t c", c=NC),
                 in0=mn[:, t0 * NC:(t0 + n) * NC].rearrange("p (t c) -> p t c", c=NC),
-                in1=fin_of[t0][:].unsqueeze(2).to_broadcast([P, n, NC]),
+                in1=x2[:, t0:t0 + n].unsqueeze(2).to_broadcast([P, n, NC]),
                 op=ALU.add,
             )
             fin_of[t0] = s
@@ -211,11 +206,15 @@ def tile_lvq_t_kernel(tc, x, prototypes, out):
             )
             nc.sync.dma_start(out=outv[:, t0 * NC:(t0 + n) * NC], in_=res[:])
 
-        load(0, 0, D)
         pr = const.tile([P, D], BF16, name="pr")
+        load(0, 0, D)
         nc.sync.dma_start(out=pr[:], in_=prototypes)
-        load(0, D, GT * D)
-        for g in range(1, LA):
+        load(0, D, 2 * D)
+        load(0, 2 * D, 3 * D)
+        load(0, 3 * D, 4 * D)
+        load(1, 0, 2 * D)
+        load(1, 2 * D, 4 * D)
+        for g in range(2, LA):
             load(g, 0, GT * D)
 
         warm = const.tile([P, 1], F32, name="warm")
@@ -226,10 +225,8 @@ def tile_lvq_t_kernel(tc, x, prototypes, out):
         make_identity(nc, ident[:])
         ones = const.tile([P, P], F32, name="ones")
         nc.vector.memset(ones[:], 1.0)
-        x2s = const.tile([P, NT], F32, name="x2s")
-        nc.vector.memset(x2s[:], 0.0)
-        x2v = const.tile([P, NT], F32, name="x2v")
-        nc.vector.memset(x2v[:], 0.0)
+        x2 = const.tile([P, NT], F32, name="x2")
+        x2part = const.tile([P, 1], F32, name="x2part")
         mn = const.tile([P, NT * NC], F32, name="mn")
         p2 = const.tile([P, 1], F32, name="p2")
         p2rep = const.tile([P, P], F32, name="p2rep")
@@ -267,6 +264,8 @@ def tile_lvq_t_kernel(tc, x, prototypes, out):
                 ]
                 for g in (a, b):
                     sb = scalar_banks(g)
+                    if g == b and k == 1:
+                        nc.vector.tensor_copy(out=p2b[:], in_=p2t[:])
                     if g == b and k >= 1:
                         stt_x(a - 2)
                     if g == 1:
@@ -288,10 +287,10 @@ def tile_lvq_t_kernel(tc, x, prototypes, out):
                 ports.append((fin_d, ab_at[k - 1]))
                 done_d.append(ab_at[k - 1])
             if k in ab_at:
-                ports.extend([(fin_a0, ab_at[k]), (fin_a1, ab_at[k]), (fin_b, ab_at[k])])
+                ports.extend([(fin_a1, ab_at[k]), (fin_b, ab_at[k])])
                 done_ab.append(ab_at[k])
             if k - 1 in GSQ_PAIRS:
-                gsq_red(a - 2, x2v[:, (a - 2) * GT + 1:(a - 2) * GT + 2])
+                gsq_red(a - 2, x2[:, (a - 2) * GT + 1:(a - 2) * GT + 2])
             if k == NK:
                 for (f, bt) in ports:
                     f(*bt)
@@ -302,20 +301,19 @@ def tile_lvq_t_kernel(tc, x, prototypes, out):
                 stt_x(b - 2)
             if k - 1 in GRAM_PAIRS:
                 diag_x(b - 2)
+            if k == GRAM_PART + 2:
+                c = (2 * GRAM_PART + 1) * GT
+                nc.vector.tensor_tensor(out=x2[:, c:c + 1], in0=x2[:, c:c + 1], in1=x2part[:], op=ALU.add)
             if k == 0:
                 nc.vector.quantize_mx(out=pcodes[:].bitcast(FP8X4), scales=pscl[:], in_=pgrp[:])
                 gsq_red("p", p2[:])
                 nc.vector.tensor_scalar_mul(out=p2rep[:], in0=ones[:], scalar1=p2[:, 0:1])
-                p2t = pgram.tile([P, P], F32, name="gram", tag="gram")
-                nc.tensor.transpose(p2t[:], p2rep[:], ident[:])
             if k < NK:
                 for (f, bt) in ports[0:1]:
                     f(*bt)
                 q_x(a)
                 for (f, bt) in ports[1:2]:
                     f(*bt)
-                if k == 0:
-                    nc.vector.tensor_copy(out=p2b[:], in_=p2t[:])
                 q_x(b)
                 for (f, bt) in ports[2:]:
                     f(*bt)
@@ -323,6 +321,9 @@ def tile_lvq_t_kernel(tc, x, prototypes, out):
                     gram_x(b)
                 mx_x(a)
                 mx_x(b)
+                if k == 0:
+                    p2t = pgram.tile([P, P], F32, name="gram", tag="gram")
+                    nc.tensor.transpose(p2t[:], p2rep[:], ident[:])
                 if k + 1 in GSQ_PAIRS:
                     gate_x(b)
                     gsq_x(a + 2, xs_of[a + 2][:, D:2 * D])
@@ -332,7 +333,6 @@ def tile_lvq_t_kernel(tc, x, prototypes, out):
         rest = [(t0, n) for (t0, n, it) in BATCHES]
         for bt in rest:
             if bt not in done_ab:
-                fin_a0(*bt)
                 fin_a1(*bt)
                 fin_b(*bt)
             if bt not in done_c:

@@ -28,10 +28,10 @@ FLOPS = 2 * B * NP * D
 TINY = 2.0 ** -116
 SQRT_TINY = 2.0 ** -58
 
-BATCHES = [(0, 48, 7), (48, 48, 13), (96, 16, 15), (112, 16, 17)]
+BATCHES = [(0, 48, 7), (48, 48, 13), (96, 24, 16)]
 GRAM_PAIRS = [1, 2, 3, 4, 5, 6, 8, 9, 10, 11, 12, 13, 14]
 GRAM_PART = 3
-S_TWO = list(range(5, NG, 6)) + [30, 31]
+S_TWO = list(range(5, NG, 3)) + [30, 31]
 GSQ_PAIRS = range(1, NK)
 
 
@@ -292,11 +292,11 @@ def tile_lvq_t_kernel(tc, x, prototypes, out):
             if k - 1 in GSQ_PAIRS:
                 gsq_red(a - 2, x2[:, (a - 2) * GT + 1:(a - 2) * GT + 2])
             if k == NK:
-                for (f, bt) in ports:
-                    f(*bt)
-                ports = []
+                fin_a1(96, 24)
             if k == NK:
                 stt_x(a - 2)
+                fin_b(96, 24)
+                fin_c(96, 24)
             if k >= 1:
                 stt_x(b - 2)
             if k - 1 in GRAM_PAIRS:
@@ -327,16 +327,28 @@ def tile_lvq_t_kernel(tc, x, prototypes, out):
                 if k + 1 in GSQ_PAIRS:
                     gate_x(b)
                     gsq_x(a + 2, xs_of[a + 2][:, D:2 * D])
-            if k >= 1:
+            if k == NK:
+                for i in range(2):
+                    nc.vector.tensor_reduce(
+                        out=mn[:, (a - 2 + i) * GT * NC:(a - 1 + i) * GT * NC],
+                        in_=tt_of[k - 1][:, i * 512:(i + 1) * 512].rearrange("p (m q) -> p m q", q=PPC),
+                        axis=AX.X,
+                        op=ALU.min,
+                    )
+            elif k >= 1:
                 red_x(k - 1)
 
-        rest = [(t0, n) for (t0, n, it) in BATCHES]
-        for bt in rest:
-            if bt not in done_ab:
-                fin_a1(*bt)
-                fin_b(*bt)
-            if bt not in done_c:
-                fin_c(*bt)
-        for bt in rest:
-            if bt not in done_d:
-                fin_d(*bt)
+        s = fin.tile([P, 8 * NC], F32, name="s", tag="s")
+        fin_of[120] = s
+        for i in range(2):
+            nc.vector.tensor_tensor(
+                out=s[:, i * 64:(i + 1) * 64].rearrange("p (t c) -> p t c", c=NC),
+                in0=mn[:, 120 * NC + i * 64:120 * NC + (i + 1) * 64].rearrange("p (t c) -> p t c", c=NC),
+                in1=x2[:, 120 + 4 * i:124 + 4 * i].unsqueeze(2).to_broadcast([P, 4, NC]),
+                op=ALU.add,
+            )
+        for i in range(2):
+            nc.vector.tensor_scalar_max(out=s[:, i * 64:(i + 1) * 64], in0=s[:, i * 64:(i + 1) * 64], scalar1=TINY)
+        fin_d(96, 24)
+        fin_c(120, 8)
+        fin_d(120, 8)

@@ -20,8 +20,8 @@ NG = NT // GT
 NK = NG // 2
 W = D // 2
 LA = 6
-XT = 5
-GW = 128
+XT = 4
+GW = 256
 
 FLOPS = 2 * B * NP * D
 
@@ -48,7 +48,7 @@ def tile_lvq_t_kernel(tc, x, prototypes, out):
         fin = ctx.enter_context(tc.tile_pool(name="fin", bufs=2))
         pxt = ctx.enter_context(tc.psum_pool(name="pxt", bufs=XT))
         pgram = ctx.enter_context(tc.psum_pool(name="pgram", bufs=1))
-        pacc = ctx.enter_context(tc.psum_pool(name="pacc", bufs=2))
+        pacc = ctx.enter_context(tc.psum_pool(name="pacc", bufs=3))
         ctx.enter_context(tc.manual_schedule())
 
         xs_of, xt_of, grp_of, mx_of, acc_of, tt_of, fin_of, gram_of, gsq_of = {}, {}, {}, {}, {}, {}, {}, {}, {}
@@ -175,7 +175,7 @@ def tile_lvq_t_kernel(tc, x, prototypes, out):
             gsq = gpool.tile([P, D], F32, name="gsq", tag="gsq")
             gsq_of[key] = gsq
             nc.gpsimd.tensor_tensor(out=gsq[:], in0=src, in1=src, op=ALU.mult)
-            for n in (512, 256, GW):
+            for n in (512, GW):
                 nc.gpsimd.tensor_tensor(out=gsq[:, 0:n], in0=gsq[:, 0:n], in1=gsq[:, n:2 * n], op=ALU.add)
 
         def gsq_red(key, col):

from contextlib import ExitStack

import concourse.mybir as mybir
from concourse.masks import make_identity

F32 = mybir.dt.float32
BF16 = mybir.dt.bfloat16
U32 = mybir.dt.uint32
U8 = mybir.dt.uint8
FP8X4 = mybir.dt.float8_e4m3fn_x4
ALU = mybir.AluOpType
ACT = mybir.ActivationFunctionType
AX = mybir.AxisListType

B, D, NP, NC, PPC = 16384, 1024, 128, 16, 8
P = 128
NT = B // P
GT = 4
NG = NT // GT
NK = NG // 2
W = D // 2
LA = 6
XT = 4
GW = 256

FLOPS = 2 * B * NP * D

TINY = 2.0 ** -116
SQRT_TINY = 2.0 ** -58

BATCHES = [(0, 48, 7), (48, 48, 13), (96, 24, 16)]
GRAM_PAIRS = [1, 2, 3, 4, 5, 6, 8, 9, 10, 11, 12, 13, 14]
GRAM_PART = 3
S_TWO = list(range(5, NG, 3)) + [30, 31]
GSQ_PAIRS = range(1, NK)


def tile_lvq_t_kernel(tc, x, prototypes, out):
    nc = tc.nc
    xv = x.rearrange("(p t) k -> p (t k)", t=NT)
    outv = out.rearrange("(p t) c -> p (t c)", t=NT)

    with ExitStack() as ctx:
        const = ctx.enter_context(tc.tile_pool(name="const", bufs=1))
        xpool = ctx.enter_context(tc.tile_pool(name="xpool", bufs=8))
        work = ctx.enter_context(tc.tile_pool(name="work", bufs=4))
        gpool = ctx.enter_context(tc.tile_pool(name="gpool", bufs=2))
        fin = ctx.enter_context(tc.tile_pool(name="fin", bufs=2))
        pxt = ctx.enter_context(tc.psum_pool(name="pxt", bufs=XT))
        pgram = ctx.enter_context(tc.psum_pool(name="pgram", bufs=1))
        pacc = ctx.enter_context(tc.psum_pool(name="pacc", bufs=3))
        ctx.enter_context(tc.manual_schedule())

        xs_of, xt_of, grp_of, mx_of, acc_of, tt_of, fin_of, gram_of, gsq_of = {}, {}, {}, {}, {}, {}, {}, {}, {}
        stream = {"live": 0, "next": 0}

        def scalar_banks(g):
            if g == 0:
                return []
            return [3, 2] if g in S_TWO else [3]

        def load(g, c0, c1):
            if g not in xs_of:
                xs_of[g] = xpool.tile([P, GT * D], BF16, name="xs", tag="xs")
            nc.sync.dma_start(out=xs_of[g][:, c0:c1], in_=xv[:, g * GT * D + c0:g * GT * D + c1])

        def transpose_words(src32, dst):
            for q in range(4):
                nc.tensor.transpose(dst[:, q * P:(q + 1) * P], src32[:, q * P:(q + 1) * P], ident[:])

        def evacuate(copy, dst32, src):
            copy(
                out=dst32.rearrange("p (g b u) -> p g b u", g=2, u=2),
                in_=src.rearrange("p (g u b) -> p g b u", g=2, u=2),
            )

        def pump():
            while stream["next"] < NT and stream["live"] < XT:
                t = stream["next"]
                xt = pxt.tile([P, W], F32, name="xt", tag="xt")
                xt_of[t] = xt
                transpose_words(xs_of[t // GT][:].bitcast(F32)[:, (t % GT) * W:(t % GT + 1) * W], xt)
                stream["next"] = t + 1
                stream["live"] = stream["live"] + 1

        def e_x(g, j):
            if g not in grp_of:
                grp_of[g] = work.tile([P, GT * D], BF16, name="grp", tag="grp", align_bytes=64)
            evacuate(
                nc.scalar.copy if j in scalar_banks(g) else nc.vector.tensor_copy,
                grp_of[g][:].bitcast(F32)[:, j * W:(j + 1) * W],
                xt_of[g * GT + j][:],
            )
            stream["live"] = stream["live"] - 1
            pump()

        def sq_x(g, j, c0=0):
            t = g * GT + j
            junk = work.tile([P, D], BF16, name="junk", tag="junk")
            nc.scalar.activation(
                out=junk[:, c0:D], in_=xs_of[g][:, j * D + c0:(j + 1) * D], func=ACT.Square, accum_out=(x2[:, t:t + 1] if c0 == 0 else x2part[:])
            )

        def q_x(g):
            codes = work.tile([P, GT * D // 4], U32, name="codes", tag="codes", align_bytes=64)
            scl = work.tile([P, GT * D // 4], U8, name="scl", tag="scl", align_bytes=64)
            mx_of[g] = (codes, scl)
            nc.vector.quantize_mx(out=codes[:].bitcast(FP8X4), scales=scl[:], in_=grp_of[g][:])

        def mx_x(g):
            codes, scl = mx_of[g]
            acc = pacc.tile([P, GT * NP], F32, name="acc", tag="acc")
            acc_of[g] = acc
            for j in range(GT):
                for h in range(2):
                    c0 = (j * 2 + h) * P
                    nc.tensor.matmul_mx(
                        out=acc[:, j * NP:(j + 1) * NP],
                        lhsT=codes[:, c0:c0 + P].bitcast(FP8X4),
                        lhsT_scale=scl[:, c0:c0 + P],
                        rhs=pcodes[:, h * NP:(h + 1) * NP].bitcast(FP8X4),
                        rhs_scale=pscl[:, h * NP:(h + 1) * NP],
                        start=(h == 0),
                        stop=(h == 1),
                    )

        def stt_x(g):
            if g % 2 == 0:
                tt_of[g // 2] = work.tile([P, 2 * GT * NP], F32, name="tt", tag="tt")
            c0 = g % 2 * GT * NP
            nc.vector.scalar_tensor_tensor(
                out=tt_of[g // 2][:, c0:c0 + GT * NP].rearrange("p (j n) -> p j n", j=GT),
                in0=acc_of[g][:].rearrange("p (j n) -> p j n", j=GT),
                scalar=-2.0,
                in1=p2b[:].unsqueeze(1).to_broadcast([P, GT, NP]),
                op0=ALU.mult,
                op1=ALU.add,
            )

        def red_x(k):
            nc.vector.tensor_reduce(
                out=mn[:, 2 * k * GT * NC:2 * (k + 1) * GT * NC],
                in_=tt_of[k][:].rearrange("p (m q) -> p m q", q=PPC),
                axis=AX.X,
                op=ALU.min,
            )

        def gram_x(g):
            gram = pgram.tile([P, P], F32, name="gram", tag="gram")
            gram_of[g] = gram
            gv = grp_of[g][:].rearrange("p (j h b t) -> p j h b t", j=GT, h=2, t=4)
            n = 6 if g // 2 == GRAM_PART else 8
            for i in range(n):
                sl = gv[:, 0, i // 4, :, i % 4]
                nc.tensor.matmul(out=gram[:], lhsT=sl, rhs=sl, start=(i == 0), stop=(i == n - 1))

        def diag_x(g):
            t = g * GT
            gj = work.tile([P, P], F32, name="gj", tag="gj")
            nc.vector.scalar_tensor_tensor(
                out=gj[:],
                in0=gram_of[g][:],
                scalar=1.0,
                in1=ident[:],
                op0=ALU.mult,
                op1=ALU.mult,
                accum_out=x2[:, t:t + 1],
            )

        def gate_x(g):
            gg = gpool.tile([P, 1], F32, name="gg", tag="gg")
            nc.gpsimd.tensor_copy(out=gg[:], in_=mx_of[g][0][:, 0:1].bitcast(F32))

        def gsq_x(key, src):
            gsq = gpool.tile([P, D], F32, name="gsq", tag="gsq")
            gsq_of[key] = gsq
            nc.gpsimd.tensor_tensor(out=gsq[:], in0=src, in1=src, op=ALU.mult)
            for n in (512, GW):
                nc.gpsimd.tensor_tensor(out=gsq[:, 0:n], in0=gsq[:, 0:n], in1=gsq[:, n:2 * n], op=ALU.add)

        def gsq_red(key, col):
            nc.vector.tensor_reduce(out=col, in_=gsq_of[key][:, 0:GW], axis=AX.X, op=ALU.add)

        def fin_a1(t0, n):
            s = fin.tile([P, n * NC], F32, name="s", tag="s")
            nc.vector.tensor_tensor(
                out=s[:].rearrange("p (t c) -> p t c", c=NC),
                in0=mn[:, t0 * NC:(t0 + n) * NC].rearrange("p (t c) -> p t c", c=NC),
                in1=x2[:, t0:t0 + n].unsqueeze(2).to_broadcast([P, n, NC]),
                op=ALU.add,
            )
            fin_of[t0] = s

        def fin_b(t0, n):
            nc.vector.tensor_scalar_max(out=fin_of[t0][:], in0=fin_of[t0][:], scalar1=TINY)

        def fin_c(t0, n):
            r = fin.tile([P, n * NC], F32, name="r", tag="r")
            nc.scalar.activation(out=r[:], in_=fin_of[t0][:], func=ACT.Sqrt)
            fin_of[t0] = r

        def fin_d(t0, n):
            res = fin.tile([P, n * NC], F32, name="res", tag="res")
            nc.vector.tensor_scalar(
                out=res[:], in0=fin_of[t0][:], scalar1=SQRT_TINY, scalar2=-1.0, op0=ALU.subtract, op1=ALU.mult
            )
            nc.sync.dma_start(out=outv[:, t0 * NC:(t0 + n) * NC], in_=res[:])

        pr = const.tile([P, D], BF16, name="pr")
        load(0, 0, D)
        nc.sync.dma_start(out=pr[:], in_=prototypes)
        load(0, D, 2 * D)
        load(0, 2 * D, 3 * D)
        load(0, 3 * D, 4 * D)
        load(1, 0, 2 * D)
        load(1, 2 * D, 4 * D)
        for g in range(2, LA):
            load(g, 0, GT * D)

        warm = const.tile([P, 1], F32, name="warm")
        nc.vector.memset(warm[:], 1.0)
        warm2 = const.tile([P, 1], F32, name="warm2")
        nc.scalar.activation(out=warm2[:], in_=warm[:], func=ACT.Sqrt)
        ident = const.tile([P, P], F32, name="ident")
        make_identity(nc, ident[:])
        ones = const.tile([P, P], F32, name="ones")
        nc.vector.memset(ones[:], 1.0)
        x2 = const.tile([P, NT], F32, name="x2")
        x2part = const.tile([P, 1], F32, name="x2part")
        mn = const.tile([P, NT * NC], F32, name="mn")
        p2 = const.tile([P, 1], F32, name="p2")
        p2rep = const.tile([P, P], F32, name="p2rep")
        p2b = const.tile([P, P], F32, name="p2b")
        pgrp = const.tile([P, D], BF16, name="pgrp", align_bytes=64)
        pcodes = const.tile([P, D // 4], U32, name="pcodes", align_bytes=64)
        pscl = const.tile([P, D // 4], U8, name="pscl", align_bytes=64)

        gsq_x("p", pr[:])

        stream["live"] = XT - 1
        pump()
        pxtile = pxt.tile([P, W], F32, name="xt", tag="xt")
        transpose_words(pr[:].bitcast(F32), pxtile)
        stream["live"] = 2
        pump()

        ab_at = dict((it, (t0, n)) for (t0, n, it) in BATCHES)
        done_ab, done_c, done_d = [], [], []

        for k in range(NK + 1):
            a, b = 2 * k, 2 * k + 1
            for g in (a + LA, b + LA):
                if g < NG:
                    load(g, 0, GT * D)
            if k - 1 in ab_at and k < NK:
                fin_c(*ab_at[k - 1])
                done_c.append(ab_at[k - 1])
            if k < NK:
                squares = [
                    (g, j)
                    for g in (a, b)
                    for j in range(GT)
                    if not ((g == b and j == 0 and k in GRAM_PAIRS) or (g == a and j == 1 and k in GSQ_PAIRS))
                ]
                for g in (a, b):
                    sb = scalar_banks(g)
                    if g == b and k == 1:
                        nc.vector.tensor_copy(out=p2b[:], in_=p2t[:])
                    if g == b and k >= 1:
                        stt_x(a - 2)
                    if g == 1:
                        for (g2, j2) in squares[2:5]:
                            sq_x(g2, j2)
                        squares = squares[0:2] + squares[5:]
                    for j in sb + [j for j in range(GT) if j not in sb]:
                        e_x(g, j)
                        if g == 0 and j == 0:
                            evacuate(nc.vector.tensor_copy, pgrp[:].bitcast(F32), pxtile[:])
                            stream["live"] = stream["live"] - 1
                            pump()
                    for (g2, j2) in (squares[0:2] if g == a else squares[2:]):
                        sq_x(g2, j2)
                    if g == b and k == GRAM_PART:
                        sq_x(b, 0, 768)
            ports = []
            if k - 1 in ab_at and ab_at[k - 1] in done_c:
                ports.append((fin_d, ab_at[k - 1]))
                done_d.append(ab_at[k - 1])
            if k in ab_at:
                ports.extend([(fin_a1, ab_at[k]), (fin_b, ab_at[k])])
                done_ab.append(ab_at[k])
            if k - 1 in GSQ_PAIRS:
                gsq_red(a - 2, x2[:, (a - 2) * GT + 1:(a - 2) * GT + 2])
            if k == NK:
                fin_a1(96, 24)
            if k == NK:
                stt_x(a - 2)
                fin_b(96, 24)
                fin_c(96, 24)
            if k >= 1:
                stt_x(b - 2)
            if k - 1 in GRAM_PAIRS:
                diag_x(b - 2)
            if k == GRAM_PART + 2:
                c = (2 * GRAM_PART + 1) * GT
                nc.vector.tensor_tensor(out=x2[:, c:c + 1], in0=x2[:, c:c + 1], in1=x2part[:], op=ALU.add)
            if k == 0:
                nc.vector.quantize_mx(out=pcodes[:].bitcast(FP8X4), scales=pscl[:], in_=pgrp[:])
                gsq_red("p", p2[:])
                nc.vector.tensor_scalar_mul(out=p2rep[:], in0=ones[:], scalar1=p2[:, 0:1])
            if k < NK:
                for (f, bt) in ports[0:1]:
                    f(*bt)
                q_x(a)
                for (f, bt) in ports[1:2]:
                    f(*bt)
                q_x(b)
                for (f, bt) in ports[2:]:
                    f(*bt)
                if k in GRAM_PAIRS:
                    gram_x(b)
                mx_x(a)
                mx_x(b)
                if k == 0:
                    p2t = pgram.tile([P, P], F32, name="gram", tag="gram")
                    nc.tensor.transpose(p2t[:], p2rep[:], ident[:])
                if k + 1 in GSQ_PAIRS:
                    gate_x(b)
                    gsq_x(a + 2, xs_of[a + 2][:, D:2 * D])
            if k == NK:
                for i in range(2):
                    nc.vector.tensor_reduce(
                        out=mn[:, (a - 2 + i) * GT * NC:(a - 1 + i) * GT * NC],
                        in_=tt_of[k - 1][:, i * 512:(i + 1) * 512].rearrange("p (m q) -> p m q", q=PPC),
                        axis=AX.X,
                        op=ALU.min,
                    )
            elif k >= 1:
                red_x(k - 1)

        s = fin.tile([P, 8 * NC], F32, name="s", tag="s")
        fin_of[120] = s
        for i in range(2):
            nc.vector.tensor_tensor(
                out=s[:, i * 64:(i + 1) * 64].rearrange("p (t c) -> p t c", c=NC),
                in0=mn[:, 120 * NC + i * 64:120 * NC + (i + 1) * 64].rearrange("p (t c) -> p t c", c=NC),
                in1=x2[:, 120 + 4 * i:124 + 4 * i].unsqueeze(2).to_broadcast([P, 4, NC]),
                op=ALU.add,
            )
        for i in range(2):
            nc.vector.tensor_scalar_max(out=s[:, i * 64:(i + 1) * 64], in0=s[:, i * 64:(i + 1) * 64], scalar1=TINY)
        fin_d(96, 24)
        fin_c(120, 8)
        fin_d(120, 8)
